import numpy as np
import ml_dtypes


def mxq(x, axis, fmt="e4m3"):
    dtype, down = {"e4m3": (ml_dtypes.float8_e4m3fn, 7), "e5m2": (ml_dtypes.float8_e5m2, 14)}[fmt]
    v = np.moveaxis(np.asarray(x, np.float32).astype(ml_dtypes.bfloat16).astype(np.float64), axis, -1)
    blocks = v.reshape(v.shape[:-1] + (-1, 32))
    amax = np.abs(blocks).max(-1, keepdims=True)
    byte = np.maximum(np.where(amax > 0, np.frexp(amax)[1] - 1 + 127, 0) - down, 1)
    scale = np.exp2(byte - 127.0)
    codes = (blocks / scale).astype(np.float32).astype(dtype).astype(np.float64)
    return np.moveaxis((codes * scale).reshape(v.shape), -1, axis)


WIDE = False


def mx_kscale(k):
    if not WIDE:
        return np.ones(k)
    levels = np.array([10, -10, 5, -5, 0])
    a = np.random.permutation(np.resize(levels, k // 512 * 4)).reshape(k // 512, 4)
    idx = np.arange(k)
    return np.exp2(a[idx // 512, idx % 128 // 32])


BF16 = ml_dtypes.bfloat16


def bf(x):
    return np.asarray(x, np.float32).astype(BF16)


def f64(x):
    return np.asarray(x).astype(np.float64)


B, D_IN, H, D_OUT, DEPTH, Q = 8192, 1024, 512, 256, 3, 2


def quantum_probs(qw):
    n = qw.shape[1]
    s0r, s0i, s1r, s1i = np.ones(n), np.zeros(n), np.zeros(n), np.zeros(n)
    for d in range(qw.shape[0]):
        th = qw[d, :, 0, 0]
        ph = qw[d, :, 1, 1]
        c, s = np.cos(th), np.sin(th)
        n0r, n0i = c * s0r - s * s1r, c * s0i - s * s1i
        n1r, n1i = s * s0r + c * s1r, s * s0i + c * s1i
        cp, sp = np.cos(ph), np.sin(ph)
        s0r, s0i = n0r, n0i
        s1r, s1i = n1r * cp - n1i * sp, n1r * sp + n1i * cp
    return s0r * s0r + s0i * s0i


def setup_inputs():
    s = mx_kscale(H)
    return {"h3": bf(np.maximum(np.random.standard_normal((B, H)), 0.0) * s),
            "q2_qw": bf(np.random.standard_normal((DEPTH, H, Q, Q))),
            "q2_cw": bf(np.random.standard_normal((H, H)) * 1.4 / np.sqrt(H) / s[:, None]),
            "q2_cb": bf(np.random.standard_normal(H) * 0.3),
            "w3": bf(np.random.standard_normal((H, D_OUT)) * 1.4 / np.sqrt(H)),
            "b3": bf(np.random.standard_normal(D_OUT) * 0.3)}


def reference(h3, q2_qw, q2_cw, q2_cb, w3, b3):
    h4 = np.tanh((mxq(f64(h3), 1, "e4m3") @ mxq(f64(q2_cw), 0, "e4m3")) + f64(q2_cb) + quantum_probs(f64(q2_qw))[None, :])
    return np.maximum((mxq(h4, 1, "e4m3") @ mxq(f64(w3), 0, "e4m3")) + f64(b3), 0.0)

@@ -1,0 +1,290 @@
+from contextlib import ExitStack
+
+import concourse.mybir as mybir
+from concourse.masks import make_identity
+
+F32 = mybir.dt.float32
+BF16 = mybir.dt.bfloat16
+U32 = mybir.dt.uint32
+U8 = mybir.dt.uint8
+FP8X4 = mybir.dt.float8_e4m3fn_x4
+ALU = mybir.AluOpType
+ACT = mybir.ActivationFunctionType
+
+P = 128
+PACK = 4
+B, H, D_OUT, DEPTH = 8192, 512, 256, 3
+CHUNK = 512
+ROW_TILES = CHUNK // P
+N_CHUNKS = B // CHUNK
+LEAD = 4
+
+FLOPS = 2 * B * H * (H + D_OUT)
+
+TWO_PI_1 = 6.28125
+TWO_PI_2 = 0.0019350051879882812
+TWO_PI_3 = 3.019916050561733e-07
+HALF_PI_HI = 1.5707963705062866
+HALF_PI_LO = -4.371138828673793e-08
+INV_TWO_PI = 0.15915493667125702
+ROUND_MAGIC = 12582912.0
+PI_BELOW = 3.141592502593994
+
+
+def hidden_bias(nc, small, qw_raw, cb_raw):
+    picked = qw_raw[:, :, :, 0:4:3].rearrange("p d t a -> p d a t")
+    angle = small.tile([P, 2, DEPTH, 2, PACK], F32)
+    nc.vector.tensor_scalar(
+        out=angle[:, 0], in0=picked, scalar1=HALF_PI_HI, scalar2=HALF_PI_LO, op0=ALU.add, op1=ALU.add
+    )
+    nc.vector.tensor_copy(out=angle[:, 1], in_=picked)
+    flat = "p s d a t -> p (s d a t)"
+    n_angles = 2 * DEPTH * 2 * PACK
+    x = angle[:].rearrange(flat)
+    shifted = small.tile([P, n_angles], F32)
+    nc.vector.tensor_scalar(
+        out=shifted[:], in0=x, scalar1=INV_TWO_PI, scalar2=ROUND_MAGIC, op0=ALU.mult, op1=ALU.add
+    )
+    turns = small.tile([P, n_angles], F32)
+    nc.vector.tensor_scalar_sub(out=turns[:], in0=shifted[:], scalar1=ROUND_MAGIC)
+    less_1 = small.tile([P, n_angles], F32)
+    nc.vector.scalar_tensor_tensor(
+        out=less_1[:], in0=turns[:], scalar=-TWO_PI_1, in1=x, op0=ALU.mult, op1=ALU.add
+    )
+    less_2 = small.tile([P, n_angles], F32)
+    nc.vector.scalar_tensor_tensor(
+        out=less_2[:], in0=turns[:], scalar=-TWO_PI_2, in1=less_1[:], op0=ALU.mult, op1=ALU.add
+    )
+    less_3 = small.tile([P, n_angles], F32)
+    nc.vector.scalar_tensor_tensor(
+        out=less_3[:], in0=turns[:], scalar=-TWO_PI_3, in1=less_2[:], op0=ALU.mult, op1=ALU.add
+    )
+    reduced = small.tile([P, n_angles], F32)
+    nc.vector.tensor_scalar(
+        out=reduced[:], in0=less_3[:], scalar1=PI_BELOW, scalar2=-PI_BELOW, op0=ALU.min, op1=ALU.max
+    )
+    trig = small.tile([P, 2, DEPTH, 2, PACK], F32)
+    nc.scalar.activation(out=trig[:].rearrange(flat), in_=reduced[:], func=ACT.Sin)
+    warm = small.tile([P, 1], F32)
+    nc.scalar.activation(out=warm[:], in_=trig[:, 0, 0, 0, 0:1], func=ACT.Tanh)
+
+    cb_f32 = small.tile([P, PACK], F32)
+    nc.vector.tensor_copy(out=cb_f32[:], in_=cb_raw[:])
+
+    amp = small.tile([P, DEPTH, 2, 2, PACK], F32)
+    nc.gpsimd.memset(amp[:, 0], 0.0)
+    nc.gpsimd.memset(amp[:, 0, 0, 0, :], 1.0)
+    by_theta = small.tile([P, DEPTH, 2, 4, PACK], F32)
+    by_phi = small.tile([P, DEPTH, 2, 2, PACK], F32)
+    turned = small.tile([P, DEPTH, 2, PACK], F32)
+    last = small.tile([P, 2, PACK], F32)
+    for d in range(DEPTH):
+        nc.gpsimd.tensor_tensor(
+            out=by_theta[:, d],
+            in0=amp[:, d].rearrange("p a c t -> p (a c) t").unsqueeze(1).to_broadcast([P, 2, 4, PACK]),
+            in1=trig[:, :, d, 0, :].unsqueeze(2).to_broadcast([P, 2, 4, PACK]),
+            op=ALU.mult,
+        )
+        next_a0 = last[:] if d == DEPTH - 1 else amp[:, d + 1, 0]
+        nc.gpsimd.tensor_tensor(
+            out=next_a0, in0=by_theta[:, d, 0, 0:2, :], in1=by_theta[:, d, 1, 2:4, :], op=ALU.subtract
+        )
+        if d < DEPTH - 1:
+            nc.gpsimd.tensor_tensor(
+                out=turned[:, d], in0=by_theta[:, d, 1, 0:2, :], in1=by_theta[:, d, 0, 2:4, :], op=ALU.add
+            )
+            nc.gpsimd.tensor_tensor(
+                out=by_phi[:, d],
+                in0=turned[:, d].unsqueeze(1).to_broadcast([P, 2, 2, PACK]),
+                in1=trig[:, :, d, 1, :].unsqueeze(2).to_broadcast([P, 2, 2, PACK]),
+                op=ALU.mult,
+            )
+            nc.gpsimd.tensor_tensor(
+                out=amp[:, d + 1, 1, 0, :], in0=by_phi[:, d, 0, 0, :], in1=by_phi[:, d, 1, 1, :], op=ALU.subtract
+            )
+            nc.gpsimd.tensor_tensor(
+                out=amp[:, d + 1, 1, 1, :], in0=by_phi[:, d, 1, 0, :], in1=by_phi[:, d, 0, 1, :], op=ALU.add
+            )
+    squares = small.tile([P, 2, PACK], F32)
+    nc.gpsimd.tensor_tensor(out=squares[:], in0=last[:], in1=last[:], op=ALU.mult)
+    prob = small.tile([P, PACK], F32)
+    nc.gpsimd.tensor_tensor(out=prob[:], in0=squares[:, 0, :], in1=squares[:, 1, :], op=ALU.add)
+    bias = small.tile([P, PACK], F32)
+    nc.gpsimd.tensor_tensor(out=bias[:], in0=prob[:], in1=cb_f32[:], op=ALU.add)
+    return bias
+
+
+def tile_quantumneuralnetwork_pb_t_kernel(tc, h3, q2_qw, q2_cw, q2_cb, w3, b3, out):
+    nc = tc.nc
+    with ExitStack() as ctx:
+        small = ctx.enter_context(tc.tile_pool(name="small", bufs=1))
+        weights = ctx.enter_context(tc.tile_pool(name="weights", bufs=1))
+        rows = ctx.enter_context(tc.tile_pool(name="rows", bufs=N_CHUNKS))
+        ahead = ctx.enter_context(tc.tile_pool(name="ahead", bufs=LEAD + 2))
+        work = ctx.enter_context(tc.tile_pool(name="work", bufs=3))
+        tr_ps = ctx.enter_context(tc.psum_pool(name="tr_ps", bufs=2))
+        s1_ps = ctx.enter_context(tc.psum_pool(name="s1_ps", bufs=4))
+        s2_ps = ctx.enter_context(tc.psum_pool(name="s2_ps", bufs=2))
+
+        qw_raw = small.tile([P, DEPTH, PACK, 4], BF16)
+        nc.sync.dma_start(out=qw_raw[:], in_=q2_qw.rearrange("d (p t) a b -> p d t (a b)", t=PACK))
+        cb_raw = small.tile([P, PACK], BF16)
+        nc.sync.dma_start(out=cb_raw[:], in_=q2_cb.rearrange("(p t) -> p t", t=PACK))
+        cw_raw = weights.tile([P, PACK, H], BF16)
+        nc.scalar.dma_start(
+            out=cw_raw[:].rearrange("q (u e) n -> q u (e n)", u=2),
+            in_=q2_cw.rearrange("(u q e) n -> q u (e n)", u=2, e=2),
+        )
+        w3_raw = weights.tile([P, PACK, D_OUT], BF16)
+        nc.scalar.dma_start(out=w3_raw[:], in_=w3.rearrange("(p t) n -> p t n", t=PACK))
+        b3_bf16 = weights.tile([P, D_OUT], BF16)
+        nc.scalar.dma_start(out=b3_bf16[:], in_=b3.partition_broadcast(P))
+        h3_rows = {}
+        for c in range(N_CHUNKS):
+            h3_sb = rows.tile([P, ROW_TILES * H], BF16)
+            nc.sync.dma_start(
+                out=h3_sb[:],
+                in_=h3[c * CHUNK : (c + 1) * CHUNK, :].rearrange("(p i) k -> p (i k)", i=ROW_TILES),
+            )
+            h3_rows[c] = h3_sb
+
+        ident = weights.tile([P, P], F32)
+        make_identity(nc, ident[:])
+
+        bias = hidden_bias(nc, small, qw_raw, cb_raw)
+
+        cw_grouped = weights.tile([P, PACK, P, PACK], BF16, align_bytes=64)
+        nc.vector.tensor_copy(
+            out=cw_grouped[:], in_=cw_raw[:].rearrange("q k (c t) -> q t c k", t=PACK)
+        )
+        cw_codes = weights.tile([P, H], U32, align_bytes=64)
+        cw_scales = weights.tile([P, H], U8, align_bytes=64)
+        w3_grouped = weights.tile([P, D_OUT, PACK], BF16, align_bytes=64)
+        nc.vector.tensor_copy(out=w3_grouped[:], in_=w3_raw[:].rearrange("p t n -> p n t"))
+        nc.vector.quantize_mx(
+            out=cw_codes[:].bitcast(FP8X4),
+            scales=cw_scales[:],
+            in_=cw_grouped[:].rearrange("q t c k -> q (t c k)"),
+        )
+        w3_codes = weights.tile([P, D_OUT], U32, align_bytes=64)
+        w3_scales = weights.tile([P, D_OUT], U8, align_bytes=64)
+        b3_f32 = weights.tile([P, D_OUT], F32)
+        nc.vector.tensor_copy(out=b3_f32[:], in_=b3_bf16[:])
+        nc.vector.quantize_mx(
+            out=w3_codes[:].bitcast(FP8X4),
+            scales=w3_scales[:],
+            in_=w3_grouped[:].rearrange("p n t -> p (n t)"),
+        )
+
+        x_grouped, x_codes, x_scales = {}, {}, {}
+        h_plain, h_grouped, h_codes, h_scales = {}, {}, {}, {}
+        sums2 = {}
+
+        def transpose_rows(c):
+            words = h3_rows[c][:].bitcast(F32)
+            grouped = work.tile([P, CHUNK * PACK], BF16, align_bytes=64, name="x_grouped")
+            grouped_words = grouped[:].bitcast(F32).rearrange("q (i b u) -> q i b u", i=ROW_TILES, u=2)
+            for half in range(2):
+                turned = tr_ps.tile([P, 2, 2, P], F32, name="turned")
+                for i in range(2):
+                    for u in range(2):
+                        start = (2 * half + i) * (H // 2) + u * P
+                        nc.tensor.transpose(turned[:, i, u, :], words[:, start : start + P], ident[:])
+                nc.scalar.copy(
+                    out=grouped_words[:, 2 * half : 2 * half + 2],
+                    in_=turned[:].rearrange("q i u b -> q i b u"),
+                )
+            x_grouped[c] = grouped
+
+        def quantise_rows(c):
+            codes = ahead.tile([P, CHUNK], U32, align_bytes=64, name="x_codes")
+            scales = ahead.tile([P, CHUNK], U8, align_bytes=64, name="x_scales")
+            nc.vector.quantize_mx(out=codes[:].bitcast(FP8X4), scales=scales[:], in_=x_grouped[c][:])
+            x_codes[c], x_scales[c] = codes, scales
+
+        def stage1(c):
+            plain = work.tile([P, PACK, CHUNK], BF16, name="h_plain")
+            for t in range(PACK):
+                sums = s1_ps.tile([P, CHUNK], F32, name="sums1")
+                nc.tensor.matmul_mx(
+                    out=sums[:],
+                    lhsT=cw_codes[:, t * P : (t + 1) * P].bitcast(FP8X4),
+                    lhsT_scale=cw_scales[:, t * P : (t + 1) * P],
+                    rhs=x_codes[c][:].bitcast(FP8X4),
+                    rhs_scale=x_scales[c][:],
+                    start=True,
+                    stop=True,
+                )
+                nc.scalar.activation(
+                    out=plain[:, t, :], in_=sums[:], func=ACT.Tanh, bias=bias[:, t : t + 1], scale=1.0
+                )
+            h_plain[c] = plain
+
+        def regroup_hidden(c):
+            grouped = work.tile([P, CHUNK, PACK], BF16, align_bytes=64, name="h_grouped")
+            nc.vector.tensor_copy(
+                out=grouped[:].rearrange("p (c i) t -> p c t i", i=4),
+                in_=h_plain[c][:].rearrange("p t (c i) -> p c t i", i=4),
+            )
+            h_grouped[c] = grouped
+
+        def quantise_hidden(c):
+            codes = work.tile([P, CHUNK], U32, align_bytes=64, name="h_codes")
+            scales = work.tile([P, CHUNK], U8, align_bytes=64, name="h_scales")
+            nc.vector.quantize_mx(
+                out=codes[:].bitcast(FP8X4),
+                scales=scales[:],
+                in_=h_grouped[c][:].rearrange("p b t -> p (b t)"),
+            )
+            h_codes[c], h_scales[c] = codes, scales
+
+        def stage2(c):
+            banks = []
+            for half in range(2):
+                sums = s2_ps.tile([P, 2, D_OUT], F32, name="sums2")
+                for i in range(2):
+                    cols = slice((2 * half + i) * P, (2 * half + i + 1) * P)
+                    nc.tensor.matmul_mx(
+                        out=sums[:, i, :],
+                        lhsT=h_codes[c][:, cols].bitcast(FP8X4),
+                        lhsT_scale=h_scales[c][:, cols],
+                        rhs=w3_codes[:].bitcast(FP8X4),
+                        rhs_scale=w3_scales[:],
+                        start=True,
+                        stop=True,
+                    )
+                banks.append(sums)
+            sums2[c] = banks
+
+        def finish(c):
+            y = work.tile([P, ROW_TILES, D_OUT], F32, name="y")
+            for half in range(2):
+                nc.vector.tensor_tensor(
+                    out=y[:, 2 * half : 2 * half + 2, :],
+                    in0=sums2[c][half][:],
+                    in1=b3_f32[:].unsqueeze(1).to_broadcast([P, 2, D_OUT]),
+                    op=ALU.add,
+                )
+            nc.vector.tensor_scalar_max(out=y[:], in0=y[:], scalar1=0.0)
+            nc.sync.dma_start(
+                out=out[c * CHUNK : (c + 1) * CHUNK, :].rearrange("(p i) n -> p i n", i=ROW_TILES),
+                in_=y[:],
+            )
+
+        for c in range(LEAD):
+            transpose_rows(c)
+            quantise_rows(c)
+        for c in range(N_CHUNKS + 1):
+            if c < N_CHUNKS:
+                stage1(c)
+            if c + LEAD < N_CHUNKS:
+                transpose_rows(c + LEAD)
+            if c < N_CHUNKS:
+                regroup_hidden(c)
+            if c + LEAD < N_CHUNKS:
+                quantise_rows(c + LEAD)
+            if c >= 1:
+                finish(c - 1)
+            if c < N_CHUNKS:
+                quantise_hidden(c)
+                stage2(c)

@@ -18,6 +18,7 @@ CHUNK = 512
 ROW_TILES = CHUNK // P
 N_CHUNKS = B // CHUNK
 LEAD = 4
+N_ANGLES = 6
 
 FLOPS = 2 * B * H * (H + D_OUT)
 
@@ -31,86 +32,88 @@ ROUND_MAGIC = 12582912.0
 PI_BELOW = 3.141592502593994
 
 
-def hidden_bias(nc, small, qw_raw, cb_raw):
-    picked = qw_raw[:, :, :, 0:4:3].rearrange("p d t a -> p d a t")
-    angle = small.tile([P, 2, DEPTH, 2, PACK], F32)
+def sines_and_cosines(nc, small, qw_raw):
+    theta = qw_raw[:, :, :, 0]
+    phi = qw_raw[:, :, :, 3]
+    angle = small.tile([P, 2, N_ANGLES, PACK], F32)
+    nc.vector.tensor_copy(out=angle[:, 1, 0:3, :], in_=theta)
+    nc.vector.tensor_copy(out=angle[:, 1, 3:6:2, :], in_=phi[:, 0:2, :])
+    nc.vector.tensor_tensor(out=angle[:, 1, 4, :], in0=phi[:, 0, :], in1=phi[:, 1, :], op=ALU.add)
     nc.vector.tensor_scalar(
-        out=angle[:, 0], in0=picked, scalar1=HALF_PI_HI, scalar2=HALF_PI_LO, op0=ALU.add, op1=ALU.add
+        out=angle[:, 0], in0=angle[:, 1], scalar1=HALF_PI_HI, scalar2=HALF_PI_LO, op0=ALU.add, op1=ALU.add
     )
-    nc.vector.tensor_copy(out=angle[:, 1], in_=picked)
-    flat = "p s d a t -> p (s d a t)"
-    n_angles = 2 * DEPTH * 2 * PACK
+    flat = "p s j t -> p (s j t)"
+    width = 2 * N_ANGLES * PACK
     x = angle[:].rearrange(flat)
-    shifted = small.tile([P, n_angles], F32)
+    shifted = small.tile([P, width], F32)
     nc.vector.tensor_scalar(
         out=shifted[:], in0=x, scalar1=INV_TWO_PI, scalar2=ROUND_MAGIC, op0=ALU.mult, op1=ALU.add
     )
-    turns = small.tile([P, n_angles], F32)
+    turns = small.tile([P, width], F32)
     nc.vector.tensor_scalar_sub(out=turns[:], in0=shifted[:], scalar1=ROUND_MAGIC)
-    less_1 = small.tile([P, n_angles], F32)
+    less_1 = small.tile([P, width], F32)
     nc.vector.scalar_tensor_tensor(
         out=less_1[:], in0=turns[:], scalar=-TWO_PI_1, in1=x, op0=ALU.mult, op1=ALU.add
     )
-    less_2 = small.tile([P, n_angles], F32)
+    less_2 = small.tile([P, width], F32)
     nc.vector.scalar_tensor_tensor(
         out=less_2[:], in0=turns[:], scalar=-TWO_PI_2, in1=less_1[:], op0=ALU.mult, op1=ALU.add
     )
-    less_3 = small.tile([P, n_angles], F32)
+    less_3 = small.tile([P, width], F32)
     nc.vector.scalar_tensor_tensor(
         out=less_3[:], in0=turns[:], scalar=-TWO_PI_3, in1=less_2[:], op0=ALU.mult, op1=ALU.add
     )
-    reduced = small.tile([P, n_angles], F32)
+    reduced = small.tile([P, width], F32)
     nc.vector.tensor_scalar(
         out=reduced[:], in0=less_3[:], scalar1=PI_BELOW, scalar2=-PI_BELOW, op0=ALU.min, op1=ALU.max
     )
-    trig = small.tile([P, 2, DEPTH, 2, PACK], F32)
+    trig = small.tile([P, 2, N_ANGLES, PACK], F32)
     nc.scalar.activation(out=trig[:].rearrange(flat), in_=reduced[:], func=ACT.Sin)
     warm = small.tile([P, 1], F32)
-    nc.scalar.activation(out=warm[:], in_=trig[:, 0, 0, 0, 0:1], func=ACT.Tanh)
+    nc.scalar.activation(out=warm[:], in_=trig[:, 0, 0, 0:1], func=ACT.Tanh)
+    return trig
 
-    cb_f32 = small.tile([P, PACK], F32)
-    nc.vector.tensor_copy(out=cb_f32[:], in_=cb_raw[:])
 
-    amp = small.tile([P, DEPTH, 2, 2, PACK], F32)
-    nc.gpsimd.memset(amp[:, 0], 0.0)
-    nc.gpsimd.memset(amp[:, 0, 0, 0, :], 1.0)
-    by_theta = small.tile([P, DEPTH, 2, 4, PACK], F32)
-    by_phi = small.tile([P, DEPTH, 2, 2, PACK], F32)
-    turned = small.tile([P, DEPTH, 2, PACK], F32)
-    last = small.tile([P, 2, PACK], F32)
-    for d in range(DEPTH):
-        nc.gpsimd.tensor_tensor(
-            out=by_theta[:, d],
-            in0=amp[:, d].rearrange("p a c t -> p (a c) t").unsqueeze(1).to_broadcast([P, 2, 4, PACK]),
-            in1=trig[:, :, d, 0, :].unsqueeze(2).to_broadcast([P, 2, 4, PACK]),
-            op=ALU.mult,
-        )
-        next_a0 = last[:] if d == DEPTH - 1 else amp[:, d + 1, 0]
-        nc.gpsimd.tensor_tensor(
-            out=next_a0, in0=by_theta[:, d, 0, 0:2, :], in1=by_theta[:, d, 1, 2:4, :], op=ALU.subtract
-        )
-        if d < DEPTH - 1:
-            nc.gpsimd.tensor_tensor(
-                out=turned[:, d], in0=by_theta[:, d, 1, 0:2, :], in1=by_theta[:, d, 0, 2:4, :], op=ALU.add
-            )
-            nc.gpsimd.tensor_tensor(
-                out=by_phi[:, d],
-                in0=turned[:, d].unsqueeze(1).to_broadcast([P, 2, 2, PACK]),
-                in1=trig[:, :, d, 1, :].unsqueeze(2).to_broadcast([P, 2, 2, PACK]),
-                op=ALU.mult,
-            )
-            nc.gpsimd.tensor_tensor(
-                out=amp[:, d + 1, 1, 0, :], in0=by_phi[:, d, 0, 0, :], in1=by_phi[:, d, 1, 1, :], op=ALU.subtract
-            )
-            nc.gpsimd.tensor_tensor(
-                out=amp[:, d + 1, 1, 1, :], in0=by_phi[:, d, 1, 0, :], in1=by_phi[:, d, 0, 1, :], op=ALU.add
-            )
-    squares = small.tile([P, 2, PACK], F32)
-    nc.gpsimd.tensor_tensor(out=squares[:], in0=last[:], in1=last[:], op=ALU.mult)
-    prob = small.tile([P, PACK], F32)
-    nc.gpsimd.tensor_tensor(out=prob[:], in0=squares[:, 0, :], in1=squares[:, 1, :], op=ALU.add)
+def hidden_bias(nc, small, trig, cb_raw):
+    to_add = small.tile([P, 3, PACK], F32)
+    nc.vector.tensor_copy(out=to_add[:, 2, :], in_=cb_raw[:])
+    pair = small.tile([P, 4, PACK], F32)
+    nc.vector.tensor_tensor(
+        out=pair[:].rearrange("p (a b) t -> p a b t", a=2),
+        in0=trig[:, :, 1, :].unsqueeze(2).to_broadcast([P, 2, 2, PACK]),
+        in1=trig[:, :, 0, :].unsqueeze(1).to_broadcast([P, 2, 2, PACK]),
+        op=ALU.mult,
+    )
+    coef = small.tile([P, 4, PACK], F32)
+    nc.vector.tensor_tensor(
+        out=coef[:, 0:2, :],
+        in0=pair[:, 0:4:3, :],
+        in1=trig[:, 0, 2, :].unsqueeze(1).to_broadcast([P, 2, PACK]),
+        op=ALU.mult,
+    )
+    nc.vector.tensor_tensor(
+        out=coef[:, 2:4, :],
+        in0=pair[:, 1:3, :],
+        in1=trig[:, 1, 2, :].unsqueeze(1).to_broadcast([P, 2, PACK]),
+        op=ALU.mult,
+    )
+    terms = small.tile([P, 2, 3, PACK], F32)
+    nc.vector.tensor_tensor(
+        out=terms[:],
+        in0=coef[:, 1:4, :].unsqueeze(1).to_broadcast([P, 2, 3, PACK]),
+        in1=trig[:, :, 3:6, :],
+        op=ALU.mult,
+    )
+    parts = small.tile([P, 2, PACK], F32)
+    nc.vector.tensor_reduce(
+        out=parts[:], in_=terms[:].rearrange("p c j t -> p c t j"), axis=mybir.AxisListType.X, op=ALU.add
+    )
+    nc.vector.tensor_tensor(out=parts[:, 0, :], in0=coef[:, 0, :], in1=parts[:, 0, :], op=ALU.subtract)
+    nc.vector.tensor_tensor(out=to_add[:, 0:2, :], in0=parts[:], in1=parts[:], op=ALU.mult)
     bias = small.tile([P, PACK], F32)
-    nc.gpsimd.tensor_tensor(out=bias[:], in0=prob[:], in1=cb_f32[:], op=ALU.add)
+    nc.vector.tensor_reduce(
+        out=bias[:], in_=to_add[:].rearrange("p j t -> p t j"), axis=mybir.AxisListType.X, op=ALU.add
+    )
     return bias
 
 
@@ -151,12 +154,13 @@ def tile_quantumneuralnetwork_pb_t_kernel(tc, h3, q2_qw, q2_cw, q2_cb, w3, b3, o
         ident = weights.tile([P, P], F32)
         make_identity(nc, ident[:])
 
-        bias = hidden_bias(nc, small, qw_raw, cb_raw)
+        trig = sines_and_cosines(nc, small, qw_raw)
 
         cw_grouped = weights.tile([P, PACK, P, PACK], BF16, align_bytes=64)
         nc.vector.tensor_copy(
             out=cw_grouped[:], in_=cw_raw[:].rearrange("q k (c t) -> q t c k", t=PACK)
         )
+        bias = hidden_bias(nc, small, trig, cb_raw)
         cw_codes = weights.tile([P, H], U32, align_bytes=64)
         cw_scales = weights.tile([P, H], U8, align_bytes=64)
         w3_grouped = weights.tile([P, D_OUT, PACK], BF16, align_bytes=64)
@@ -265,7 +269,9 @@ def tile_quantumneuralnetwork_pb_t_kernel(tc, h3, q2_qw, q2_cw, q2_cb, w3, b3, o
                     in1=b3_f32[:].unsqueeze(1).to_broadcast([P, 2, D_OUT]),
                     op=ALU.add,
                 )
-            nc.vector.tensor_scalar_max(out=y[:], in0=y[:], scalar1=0.0)
+            nc.gpsimd.tensor_scalar(
+                out=y[:], in0=y[:], scalar1=0.0, scalar2=0.0, op0=ALU.max, op1=ALU.add
+            )
             nc.sync.dma_start(
                 out=out[c * CHUNK : (c + 1) * CHUNK, :].rearrange("(p i) n -> p i n", i=ROW_TILES),
                 in_=y[:],

@@ -124,7 +124,7 @@ def tile_quantumneuralnetwork_pb_t_kernel(tc, h3, q2_qw, q2_cw, q2_cb, w3, b3, o
         weights = ctx.enter_context(tc.tile_pool(name="weights", bufs=1))
         rows = ctx.enter_context(tc.tile_pool(name="rows", bufs=N_CHUNKS))
         ahead = ctx.enter_context(tc.tile_pool(name="ahead", bufs=LEAD + 2))
-        work = ctx.enter_context(tc.tile_pool(name="work", bufs=3))
+        work = ctx.enter_context(tc.tile_pool(name="work", bufs=4))
         tr_ps = ctx.enter_context(tc.psum_pool(name="tr_ps", bufs=2))
         s1_ps = ctx.enter_context(tc.psum_pool(name="s1_ps", bufs=4))
         s2_ps = ctx.enter_context(tc.psum_pool(name="s2_ps", bufs=2))
@@ -269,9 +269,10 @@ def tile_quantumneuralnetwork_pb_t_kernel(tc, h3, q2_qw, q2_cw, q2_cb, w3, b3, o
                     in1=b3_f32[:].unsqueeze(1).to_broadcast([P, 2, D_OUT]),
                     op=ALU.add,
                 )
-            nc.gpsimd.tensor_scalar(
-                out=y[:], in0=y[:], scalar1=0.0, scalar2=0.0, op0=ALU.max, op1=ALU.add
-            )
+            if c % 2 == 0:
+                nc.scalar.activation(out=y[:], in_=y[:], func=ACT.Relu)
+            else:
+                nc.vector.tensor_scalar_max(out=y[:], in0=y[:], scalar1=0.0)
             nc.sync.dma_start(
                 out=out[c * CHUNK : (c + 1) * CHUNK, :].rearrange("(p i) n -> p i n", i=ROW_TILES),
                 in_=y[:],

@@ -17,7 +17,7 @@ B, H, D_OUT, DEPTH = 8192, 512, 256, 3
 CHUNK = 512
 ROW_TILES = CHUNK // P
 N_CHUNKS = B // CHUNK
-LEAD = 4
+LEAD = 2
 N_ANGLES = 6
 
 FLOPS = 2 * B * H * (H + D_OUT)
@@ -128,22 +128,24 @@ def tile_quantumneuralnetwork_pb_t_kernel(tc, h3, q2_qw, q2_cw, q2_cb, w3, b3, o
         tr_ps = ctx.enter_context(tc.psum_pool(name="tr_ps", bufs=2))
         s1_ps = ctx.enter_context(tc.psum_pool(name="s1_ps", bufs=4))
         s2_ps = ctx.enter_context(tc.psum_pool(name="s2_ps", bufs=2))
+        ctx.enter_context(tc.manual_schedule())
 
         qw_raw = small.tile([P, DEPTH, PACK, 4], BF16)
         nc.sync.dma_start(out=qw_raw[:], in_=q2_qw.rearrange("d (p t) a b -> p d t (a b)", t=PACK))
         cb_raw = small.tile([P, PACK], BF16)
-        nc.sync.dma_start(out=cb_raw[:], in_=q2_cb.rearrange("(p t) -> p t", t=PACK))
         cw_raw = weights.tile([P, PACK, H], BF16)
         nc.scalar.dma_start(
             out=cw_raw[:].rearrange("q (u e) n -> q u (e n)", u=2),
             in_=q2_cw.rearrange("(u q e) n -> q u (e n)", u=2, e=2),
         )
+        nc.scalar.dma_start(out=cb_raw[:], in_=q2_cb.rearrange("(p t) -> p t", t=PACK))
         w3_raw = weights.tile([P, PACK, D_OUT], BF16)
-        nc.scalar.dma_start(out=w3_raw[:], in_=w3.rearrange("(p t) n -> p t n", t=PACK))
         b3_bf16 = weights.tile([P, D_OUT], BF16)
-        nc.scalar.dma_start(out=b3_bf16[:], in_=b3.partition_broadcast(P))
         h3_rows = {}
         for c in range(N_CHUNKS):
+            if c == LEAD:
+                nc.sync.dma_start(out=w3_raw[:], in_=w3.rearrange("(p t) n -> p t n", t=PACK))
+                nc.sync.dma_start(out=b3_bf16[:], in_=b3.partition_broadcast(P))
             h3_sb = rows.tile([P, ROW_TILES * H], BF16)
             nc.sync.dma_start(
                 out=h3_sb[:],
@@ -163,26 +165,28 @@ def tile_quantumneuralnetwork_pb_t_kernel(tc, h3, q2_qw, q2_cw, q2_cb, w3, b3, o
         bias = hidden_bias(nc, small, trig, cb_raw)
         cw_codes = weights.tile([P, H], U32, align_bytes=64)
         cw_scales = weights.tile([P, H], U8, align_bytes=64)
-        w3_grouped = weights.tile([P, D_OUT, PACK], BF16, align_bytes=64)
-        nc.vector.tensor_copy(out=w3_grouped[:], in_=w3_raw[:].rearrange("p t n -> p n t"))
         nc.vector.quantize_mx(
             out=cw_codes[:].bitcast(FP8X4),
             scales=cw_scales[:],
             in_=cw_grouped[:].rearrange("q t c k -> q (t c k)"),
         )
+        w3_grouped = weights.tile([P, D_OUT, PACK], BF16, align_bytes=64)
         w3_codes = weights.tile([P, D_OUT], U32, align_bytes=64)
         w3_scales = weights.tile([P, D_OUT], U8, align_bytes=64)
         b3_f32 = weights.tile([P, D_OUT], F32)
-        nc.vector.tensor_copy(out=b3_f32[:], in_=b3_bf16[:])
-        nc.vector.quantize_mx(
-            out=w3_codes[:].bitcast(FP8X4),
-            scales=w3_scales[:],
-            in_=w3_grouped[:].rearrange("p n t -> p (n t)"),
-        )
+
+        def prepare_stage2():
+            nc.vector.tensor_copy(out=w3_grouped[:], in_=w3_raw[:].rearrange("p t n -> p n t"))
+            nc.vector.tensor_copy(out=b3_f32[:], in_=b3_bf16[:])
+            nc.vector.quantize_mx(
+                out=w3_codes[:].bitcast(FP8X4),
+                scales=w3_scales[:],
+                in_=w3_grouped[:].rearrange("p n t -> p (n t)"),
+            )
 
         x_grouped, x_codes, x_scales = {}, {}, {}
         h_plain, h_grouped, h_codes, h_scales = {}, {}, {}, {}
-        sums2 = {}
+        sums2, outputs = {}, {}
 
         def transpose_rows(c):
             words = h3_rows[c][:].bitcast(F32)
@@ -260,7 +264,7 @@ def tile_quantumneuralnetwork_pb_t_kernel(tc, h3, q2_qw, q2_cw, q2_cb, w3, b3, o
                 banks.append(sums)
             sums2[c] = banks
 
-        def finish(c):
+        def add_bias(c):
             y = work.tile([P, ROW_TILES, D_OUT], F32, name="y")
             for half in range(2):
                 nc.vector.tensor_tensor(
@@ -269,6 +273,10 @@ def tile_quantumneuralnetwork_pb_t_kernel(tc, h3, q2_qw, q2_cw, q2_cb, w3, b3, o
                     in1=b3_f32[:].unsqueeze(1).to_broadcast([P, 2, D_OUT]),
                     op=ALU.add,
                 )
+            outputs[c] = y
+
+        def relu_and_store(c):
+            y = outputs[c]
             if c % 2 == 0:
                 nc.scalar.activation(out=y[:], in_=y[:], func=ACT.Relu)
             else:
@@ -280,18 +288,25 @@ def tile_quantumneuralnetwork_pb_t_kernel(tc, h3, q2_qw, q2_cw, q2_cb, w3, b3, o
 
         for c in range(LEAD):
             transpose_rows(c)
+        for c in range(LEAD - 1):
             quantise_rows(c)
-        for c in range(N_CHUNKS + 1):
-            if c < N_CHUNKS:
-                stage1(c)
-            if c + LEAD < N_CHUNKS:
-                transpose_rows(c + LEAD)
-            if c < N_CHUNKS:
-                regroup_hidden(c)
-            if c + LEAD < N_CHUNKS:
-                quantise_rows(c + LEAD)
-            if c >= 1:
-                finish(c - 1)
-            if c < N_CHUNKS:
-                quantise_hidden(c)
-                stage2(c)
+        prepare_stage2()
+        for r in range(-1, N_CHUNKS + 1):
+            if r + 1 < N_CHUNKS:
+                stage1(r + 1)
+            if r + 1 + LEAD < N_CHUNKS:
+                transpose_rows(r + 1 + LEAD)
+            if 0 <= r - 2 and (r - 2) % 2 == 0:
+                relu_and_store(r - 2)
+            if 0 <= r - 1 < N_CHUNKS:
+                stage2(r - 1)
+            if 0 <= r < N_CHUNKS:
+                regroup_hidden(r)
+            if r + LEAD < N_CHUNKS:
+                quantise_rows(r + LEAD)
+            if 0 <= r - 1 < N_CHUNKS:
+                add_bias(r - 1)
+            if 0 <= r < N_CHUNKS:
+                quantise_hidden(r)
+            if 0 <= r - 1 < N_CHUNKS and (r - 1) % 2 == 1:
+                relu_and_store(r - 1)

@@ -18,6 +18,8 @@ CHUNK = 512
 ROW_TILES = CHUNK // P
 N_CHUNKS = B // CHUNK
 LEAD = 2
+VECTOR_COLS = 384
+SCALAR_RELU_EVERY = 4
 N_ANGLES = 6
 
 FLOPS = 2 * B * H * (H + D_OUT)
@@ -231,8 +233,16 @@ def tile_quantumneuralnetwork_pb_t_kernel(tc, h3, q2_qw, q2_cw, q2_cb, w3, b3, o
         def regroup_hidden(c):
             grouped = work.tile([P, CHUNK, PACK], BF16, align_bytes=64, name="h_grouped")
             nc.vector.tensor_copy(
-                out=grouped[:].rearrange("p (c i) t -> p c t i", i=4),
-                in_=h_plain[c][:].rearrange("p t (c i) -> p c t i", i=4),
+                out=grouped[:, 0:VECTOR_COLS, :].rearrange("p (c i) t -> p c t i", i=4),
+                in_=h_plain[c][:, :, 0:VECTOR_COLS].rearrange("p t (c i) -> p c t i", i=4),
+            )
+            nc.gpsimd.tensor_scalar(
+                out=grouped[:, VECTOR_COLS:CHUNK, :],
+                in0=h_plain[c][:, :, VECTOR_COLS:CHUNK].rearrange("p t b -> p b t"),
+                scalar1=1.0,
+                scalar2=0.0,
+                op0=ALU.mult,
+                op1=ALU.add,
             )
             h_grouped[c] = grouped
 
@@ -277,7 +287,7 @@ def tile_quantumneuralnetwork_pb_t_kernel(tc, h3, q2_qw, q2_cw, q2_cb, w3, b3, o
 
         def relu_and_store(c):
             y = outputs[c]
-            if c % 2 == 0:
+            if c % SCALAR_RELU_EVERY == 0:
                 nc.scalar.activation(out=y[:], in_=y[:], func=ACT.Relu)
             else:
                 nc.vector.tensor_scalar_max(out=y[:], in0=y[:], scalar1=0.0)
@@ -296,7 +306,7 @@ def tile_quantumneuralnetwork_pb_t_kernel(tc, h3, q2_qw, q2_cw, q2_cb, w3, b3, o
                 stage1(r + 1)
             if r + 1 + LEAD < N_CHUNKS:
                 transpose_rows(r + 1 + LEAD)
-            if 0 <= r - 2 and (r - 2) % 2 == 0:
+            if 0 <= r - 2 and (r - 2) % SCALAR_RELU_EVERY == 0:
                 relu_and_store(r - 2)
             if 0 <= r - 1 < N_CHUNKS:
                 stage2(r - 1)
@@ -308,5 +318,5 @@ def tile_quantumneuralnetwork_pb_t_kernel(tc, h3, q2_qw, q2_cw, q2_cb, w3, b3, o
                 add_bias(r - 1)
             if 0 <= r < N_CHUNKS:
                 quantise_hidden(r)
-            if 0 <= r - 1 < N_CHUNKS and (r - 1) % 2 == 1:
+            if 0 <= r - 1 < N_CHUNKS and (r - 1) % SCALAR_RELU_EVERY != 0:
                 relu_and_store(r - 1)

@@ -18,8 +18,7 @@ CHUNK = 512
 ROW_TILES = CHUNK // P
 N_CHUNKS = B // CHUNK
 LEAD = 2
-VECTOR_COLS = 384
-SCALAR_RELU_EVERY = 4
+F32_MAX = 3.4028234663852886e38
 N_ANGLES = 6
 
 FLOPS = 2 * B * H * (H + D_OUT)
@@ -233,16 +232,8 @@ def tile_quantumneuralnetwork_pb_t_kernel(tc, h3, q2_qw, q2_cw, q2_cb, w3, b3, o
         def regroup_hidden(c):
             grouped = work.tile([P, CHUNK, PACK], BF16, align_bytes=64, name="h_grouped")
             nc.vector.tensor_copy(
-                out=grouped[:, 0:VECTOR_COLS, :].rearrange("p (c i) t -> p c t i", i=4),
-                in_=h_plain[c][:, :, 0:VECTOR_COLS].rearrange("p t (c i) -> p c t i", i=4),
-            )
-            nc.gpsimd.tensor_scalar(
-                out=grouped[:, VECTOR_COLS:CHUNK, :],
-                in0=h_plain[c][:, :, VECTOR_COLS:CHUNK].rearrange("p t b -> p b t"),
-                scalar1=1.0,
-                scalar2=0.0,
-                op0=ALU.mult,
-                op1=ALU.add,
+                out=grouped[:].rearrange("p (c i) t -> p c t i", i=4),
+                in_=h_plain[c][:].rearrange("p t (c i) -> p c t i", i=4),
             )
             h_grouped[c] = grouped
 
@@ -287,10 +278,9 @@ def tile_quantumneuralnetwork_pb_t_kernel(tc, h3, q2_qw, q2_cw, q2_cb, w3, b3, o
 
         def relu_and_store(c):
             y = outputs[c]
-            if c % SCALAR_RELU_EVERY == 0:
-                nc.scalar.activation(out=y[:], in_=y[:], func=ACT.Relu)
-            else:
-                nc.vector.tensor_scalar_max(out=y[:], in0=y[:], scalar1=0.0)
+            nc.gpsimd.tensor_scalar(
+                out=y[:], in0=y[:], scalar1=F32_MAX, scalar2=0.0, op0=ALU.min, op1=ALU.max
+            )
             nc.sync.dma_start(
                 out=out[c * CHUNK : (c + 1) * CHUNK, :].rearrange("(p i) n -> p i n", i=ROW_TILES),
                 in_=y[:],
@@ -306,8 +296,6 @@ def tile_quantumneuralnetwork_pb_t_kernel(tc, h3, q2_qw, q2_cw, q2_cb, w3, b3, o
                 stage1(r + 1)
             if r + 1 + LEAD < N_CHUNKS:
                 transpose_rows(r + 1 + LEAD)
-            if 0 <= r - 2 and (r - 2) % SCALAR_RELU_EVERY == 0:
-                relu_and_store(r - 2)
             if 0 <= r - 1 < N_CHUNKS:
                 stage2(r - 1)
             if 0 <= r < N_CHUNKS:
@@ -316,7 +304,6 @@ def tile_quantumneuralnetwork_pb_t_kernel(tc, h3, q2_qw, q2_cw, q2_cb, w3, b3, o
                 quantise_rows(r + LEAD)
             if 0 <= r - 1 < N_CHUNKS:
                 add_bias(r - 1)
+                relu_and_store(r - 1)
             if 0 <= r < N_CHUNKS:
                 quantise_hidden(r)
-            if 0 <= r - 1 < N_CHUNKS and (r - 1) % SCALAR_RELU_EVERY != 0:
-                relu_and_store(r - 1)

@@ -1,3 +1,4 @@
+import math
 from contextlib import ExitStack
 
 import concourse.mybir as mybir
@@ -14,106 +15,92 @@ ACT = mybir.ActivationFunctionType
 P = 128
 PACK = 4
 B, H, D_OUT, DEPTH = 8192, 512, 256, 3
-CHUNK = 512
-ROW_TILES = CHUNK // P
-N_CHUNKS = B // CHUNK
-LEAD = 2
+CHUNK_ROWS = [256, 256] + [512] * 14 + [256, 128, 128]
+N_CHUNKS = len(CHUNK_ROWS)
+CHUNK_STARTS = [sum(CHUNK_ROWS[:c]) for c in range(N_CHUNKS)]
+TR_LEAD = 2
+Q_LEAD = 1
 F32_MAX = 3.4028234663852886e38
-N_ANGLES = 6
 
 FLOPS = 2 * B * H * (H + D_OUT)
 
-TWO_PI_1 = 6.28125
-TWO_PI_2 = 0.0019350051879882812
-TWO_PI_3 = 3.019916050561733e-07
-HALF_PI_HI = 1.5707963705062866
-HALF_PI_LO = -4.371138828673793e-08
-INV_TWO_PI = 0.15915493667125702
+INV_TWO_PI = 1.0 / (2.0 * math.pi)
 ROUND_MAGIC = 12582912.0
-PI_BELOW = 3.141592502593994
+HALF_BELOW = 0.4999999
 
 
 def sines_and_cosines(nc, small, qw_raw):
-    theta = qw_raw[:, :, :, 0]
-    phi = qw_raw[:, :, :, 3]
-    angle = small.tile([P, 2, N_ANGLES, PACK], F32)
-    nc.vector.tensor_copy(out=angle[:, 1, 0:3, :], in_=theta)
-    nc.vector.tensor_copy(out=angle[:, 1, 3:6:2, :], in_=phi[:, 0:2, :])
-    nc.vector.tensor_tensor(out=angle[:, 1, 4, :], in0=phi[:, 0, :], in1=phi[:, 1, :], op=ALU.add)
-    nc.vector.tensor_scalar(
-        out=angle[:, 0], in0=angle[:, 1], scalar1=HALF_PI_HI, scalar2=HALF_PI_LO, op0=ALU.add, op1=ALU.add
-    )
-    flat = "p s j t -> p (s j t)"
-    width = 2 * N_ANGLES * PACK
-    x = angle[:].rearrange(flat)
-    shifted = small.tile([P, width], F32)
-    nc.vector.tensor_scalar(
-        out=shifted[:], in0=x, scalar1=INV_TWO_PI, scalar2=ROUND_MAGIC, op0=ALU.mult, op1=ALU.add
-    )
-    turns = small.tile([P, width], F32)
+    angles = ((qw_raw[:, :, :, 0], 2.0 * INV_TWO_PI), (qw_raw[:, :, :, 3], INV_TWO_PI))
+    shifted = small.tile([P, 2, DEPTH, PACK], F32)
+    for a, (raw, scale) in enumerate(angles):
+        nc.vector.tensor_scalar(
+            out=shifted[:, a], in0=raw, scalar1=scale, scalar2=ROUND_MAGIC, op0=ALU.mult, op1=ALU.add
+        )
+    turns = small.tile([P, 2, DEPTH, PACK], F32)
     nc.vector.tensor_scalar_sub(out=turns[:], in0=shifted[:], scalar1=ROUND_MAGIC)
-    less_1 = small.tile([P, width], F32)
-    nc.vector.scalar_tensor_tensor(
-        out=less_1[:], in0=turns[:], scalar=-TWO_PI_1, in1=x, op0=ALU.mult, op1=ALU.add
-    )
-    less_2 = small.tile([P, width], F32)
-    nc.vector.scalar_tensor_tensor(
-        out=less_2[:], in0=turns[:], scalar=-TWO_PI_2, in1=less_1[:], op0=ALU.mult, op1=ALU.add
-    )
-    less_3 = small.tile([P, width], F32)
-    nc.vector.scalar_tensor_tensor(
-        out=less_3[:], in0=turns[:], scalar=-TWO_PI_3, in1=less_2[:], op0=ALU.mult, op1=ALU.add
-    )
-    reduced = small.tile([P, width], F32)
+    part = small.tile([P, 2, DEPTH, PACK], F32)
+    for a, (raw, scale) in enumerate(angles):
+        nc.vector.scalar_tensor_tensor(
+            out=part[:, a], in0=raw, scalar=scale, in1=turns[:, a], op0=ALU.mult, op1=ALU.subtract
+        )
+    clipped = small.tile([P, 2, DEPTH, PACK], F32)
     nc.vector.tensor_scalar(
-        out=reduced[:], in0=less_3[:], scalar1=PI_BELOW, scalar2=-PI_BELOW, op0=ALU.min, op1=ALU.max
+        out=clipped[:], in0=part[:], scalar1=HALF_BELOW, scalar2=-HALF_BELOW, op0=ALU.min, op1=ALU.max
     )
-    trig = small.tile([P, 2, N_ANGLES, PACK], F32)
-    nc.scalar.activation(out=trig[:].rearrange(flat), in_=reduced[:], func=ACT.Sin)
-    warm = small.tile([P, 1], F32)
-    nc.scalar.activation(out=warm[:], in_=trig[:, 0, 0, 0:1], func=ACT.Tanh)
+    size = small.tile([P, 2, DEPTH, PACK], F32)
+    nc.vector.scalar_tensor_tensor(
+        out=size[:], in0=part[:], scalar=-1.0, in1=part[:], op0=ALU.mult, op1=ALU.max
+    )
+    trig = small.tile([P, 2, 2, DEPTH, PACK], F32)
+    nc.scalar.activation(out=trig[:, 0], in_=clipped[:], func=ACT.Sin, scale=2.0 * math.pi)
+    nc.scalar.activation(
+        out=trig[:, 1], in_=size[:], func=ACT.Sin, scale=-2.0 * math.pi, bias=math.pi / 2
+    )
     return trig
 
 
-def hidden_bias(nc, small, trig, cb_raw):
-    to_add = small.tile([P, 3, PACK], F32)
-    nc.vector.tensor_copy(out=to_add[:, 2, :], in_=cb_raw[:])
-    pair = small.tile([P, 4, PACK], F32)
+def hidden_bias(nc, small, trig, cb_raw, between):
+    cb_half = small.tile([P, PACK], F32)
+    nc.gpsimd.tensor_scalar(
+        out=cb_half[:], in0=cb_raw[:], scalar1=1.0, scalar2=0.5, op0=ALU.mult, op1=ALU.add
+    )
+    xk = small.tile([P, 2, 2, PACK], F32)
     nc.vector.tensor_tensor(
-        out=pair[:].rearrange("p (a b) t -> p a b t", a=2),
-        in0=trig[:, :, 1, :].unsqueeze(2).to_broadcast([P, 2, 2, PACK]),
-        in1=trig[:, :, 0, :].unsqueeze(1).to_broadcast([P, 2, 2, PACK]),
+        out=xk[:],
+        in0=trig[:, 0, 0, 0:3:2, :].unsqueeze(1).to_broadcast([P, 2, 2, PACK]),
+        in1=trig[:, :, 1, 0:2, :],
         op=ALU.mult,
     )
-    coef = small.tile([P, 4, PACK], F32)
+    turn = trig[:, :, 0, 1, :]
+    by_z = small.tile([P, 2, PACK], F32)
     nc.vector.tensor_tensor(
-        out=coef[:, 0:2, :],
-        in0=pair[:, 0:4:3, :],
-        in1=trig[:, 0, 2, :].unsqueeze(1).to_broadcast([P, 2, PACK]),
-        op=ALU.mult,
+        out=by_z[:], in0=turn, in1=trig[:, 1, 0, 0, :].unsqueeze(1).to_broadcast([P, 2, PACK]), op=ALU.mult
     )
+    between[0]()
+    by_x = small.tile([P, 2, PACK], F32)
     nc.vector.tensor_tensor(
-        out=coef[:, 2:4, :],
-        in0=pair[:, 1:3, :],
-        in1=trig[:, 1, 2, :].unsqueeze(1).to_broadcast([P, 2, PACK]),
-        op=ALU.mult,
+        out=by_x[:], in0=turn, in1=xk[:, 1, 0, :].unsqueeze(1).to_broadcast([P, 2, PACK]), op=ALU.mult
     )
-    terms = small.tile([P, 2, 3, PACK], F32)
-    nc.vector.tensor_tensor(
-        out=terms[:],
-        in0=coef[:, 1:4, :].unsqueeze(1).to_broadcast([P, 2, 3, PACK]),
-        in1=trig[:, :, 3:6, :],
-        op=ALU.mult,
+    between[1]()
+    z1 = small.tile([P, PACK], F32)
+    nc.vector.tensor_tensor(out=z1[:], in0=by_z[:, 1, :], in1=by_x[:, 0, :], op=ALU.subtract)
+    minus_x1 = xk[:, 1, 0, :]
+    nc.vector.scalar_tensor_tensor(
+        out=minus_x1, in0=by_z[:, 0, :], scalar=-1.0, in1=by_x[:, 1, :], op0=ALU.mult, op1=ALU.subtract
     )
-    parts = small.tile([P, 2, PACK], F32)
+    between[2]()
+    terms = small.tile([P, 3, PACK], F32)
+    nc.vector.tensor_tensor(out=terms[:, 2, :], in0=z1[:], in1=trig[:, 1, 0, 2, :], op=ALU.mult)
+    nc.vector.tensor_tensor(out=terms[:, 0:2, :], in0=xk[:, :, 0, :], in1=xk[:, :, 1, :], op=ALU.mult)
+    between[3]()
+    z2 = small.tile([P, PACK], F32)
     nc.vector.tensor_reduce(
-        out=parts[:], in_=terms[:].rearrange("p c j t -> p c t j"), axis=mybir.AxisListType.X, op=ALU.add
+        out=z2[:], in_=terms[:].rearrange("p j t -> p t j"), axis=mybir.AxisListType.X, op=ALU.add
     )
-    nc.vector.tensor_tensor(out=parts[:, 0, :], in0=coef[:, 0, :], in1=parts[:, 0, :], op=ALU.subtract)
-    nc.vector.tensor_tensor(out=to_add[:, 0:2, :], in0=parts[:], in1=parts[:], op=ALU.mult)
+    between[4]()
     bias = small.tile([P, PACK], F32)
-    nc.vector.tensor_reduce(
-        out=bias[:], in_=to_add[:].rearrange("p j t -> p t j"), axis=mybir.AxisListType.X, op=ALU.add
+    nc.vector.scalar_tensor_tensor(
+        out=bias[:], in0=z2[:], scalar=0.5, in1=cb_half[:], op0=ALU.mult, op1=ALU.add
     )
     return bias
 
@@ -124,8 +111,9 @@ def tile_quantumneuralnetwork_pb_t_kernel(tc, h3, q2_qw, q2_cw, q2_cb, w3, b3, o
         small = ctx.enter_context(tc.tile_pool(name="small", bufs=1))
         weights = ctx.enter_context(tc.tile_pool(name="weights", bufs=1))
         rows = ctx.enter_context(tc.tile_pool(name="rows", bufs=N_CHUNKS))
-        ahead = ctx.enter_context(tc.tile_pool(name="ahead", bufs=LEAD + 2))
+        ahead = ctx.enter_context(tc.tile_pool(name="ahead", bufs=Q_LEAD + 2))
         work = ctx.enter_context(tc.tile_pool(name="work", bufs=4))
+        xg = ctx.enter_context(tc.tile_pool(name="xg", bufs=TR_LEAD + 2))
         tr_ps = ctx.enter_context(tc.psum_pool(name="tr_ps", bufs=2))
         s1_ps = ctx.enter_context(tc.psum_pool(name="s1_ps", bufs=4))
         s2_ps = ctx.enter_context(tc.psum_pool(name="s2_ps", bufs=2))
@@ -140,81 +128,84 @@ def tile_quantumneuralnetwork_pb_t_kernel(tc, h3, q2_qw, q2_cw, q2_cb, w3, b3, o
             in_=q2_cw.rearrange("(u q e) n -> q u (e n)", u=2, e=2),
         )
         nc.scalar.dma_start(out=cb_raw[:], in_=q2_cb.rearrange("(p t) -> p t", t=PACK))
+        warm = small.tile([P, 1], F32)
+        nc.gpsimd.memset(warm[:], 0.0)
+        nc.scalar.activation(out=warm[:], in_=warm[:], func=ACT.Sin)
         w3_raw = weights.tile([P, PACK, D_OUT], BF16)
         b3_bf16 = weights.tile([P, D_OUT], BF16)
         h3_rows = {}
         for c in range(N_CHUNKS):
-            if c == LEAD:
+            if c == 2:
                 nc.sync.dma_start(out=w3_raw[:], in_=w3.rearrange("(p t) n -> p t n", t=PACK))
                 nc.sync.dma_start(out=b3_bf16[:], in_=b3.partition_broadcast(P))
-            h3_sb = rows.tile([P, ROW_TILES * H], BF16)
+            tiles = CHUNK_ROWS[c] // P
+            h3_sb = rows.tile([P, tiles * H], BF16, name="h3_sb")
             nc.sync.dma_start(
                 out=h3_sb[:],
-                in_=h3[c * CHUNK : (c + 1) * CHUNK, :].rearrange("(p i) k -> p (i k)", i=ROW_TILES),
+                in_=h3[CHUNK_STARTS[c] : CHUNK_STARTS[c] + CHUNK_ROWS[c], :].rearrange(
+                    "(p i) k -> p (i k)", i=tiles
+                ),
             )
             h3_rows[c] = h3_sb
 
         ident = weights.tile([P, P], F32)
         make_identity(nc, ident[:])
 
-        trig = sines_and_cosines(nc, small, qw_raw)
-
         cw_grouped = weights.tile([P, PACK, P, PACK], BF16, align_bytes=64)
-        nc.vector.tensor_copy(
-            out=cw_grouped[:], in_=cw_raw[:].rearrange("q k (c t) -> q t c k", t=PACK)
-        )
-        bias = hidden_bias(nc, small, trig, cb_raw)
+        cw_by_pass = cw_raw[:].rearrange("q k (c t) -> q t c k", t=PACK)
         cw_codes = weights.tile([P, H], U32, align_bytes=64)
         cw_scales = weights.tile([P, H], U8, align_bytes=64)
-        nc.vector.quantize_mx(
-            out=cw_codes[:].bitcast(FP8X4),
-            scales=cw_scales[:],
-            in_=cw_grouped[:].rearrange("q t c k -> q (t c k)"),
-        )
         w3_grouped = weights.tile([P, D_OUT, PACK], BF16, align_bytes=64)
         w3_codes = weights.tile([P, D_OUT], U32, align_bytes=64)
         w3_scales = weights.tile([P, D_OUT], U8, align_bytes=64)
         b3_f32 = weights.tile([P, D_OUT], F32)
 
-        def prepare_stage2():
-            nc.vector.tensor_copy(out=w3_grouped[:], in_=w3_raw[:].rearrange("p t n -> p n t"))
-            nc.vector.tensor_copy(out=b3_f32[:], in_=b3_bf16[:])
+        def quantise_cw(first, last):
             nc.vector.quantize_mx(
-                out=w3_codes[:].bitcast(FP8X4),
-                scales=w3_scales[:],
-                in_=w3_grouped[:].rearrange("p n t -> p (n t)"),
+                out=cw_codes[:, first * P : last * P].bitcast(FP8X4),
+                scales=cw_scales[:, first * P : last * P],
+                in_=cw_grouped[:, first:last].rearrange("q t c k -> q (t c k)"),
             )
 
         x_grouped, x_codes, x_scales = {}, {}, {}
         h_plain, h_grouped, h_codes, h_scales = {}, {}, {}, {}
         sums2, outputs = {}, {}
 
-        def transpose_rows(c):
+        def transpose_bank(c, bank, copy):
+            tiles = CHUNK_ROWS[c] // P
             words = h3_rows[c][:].bitcast(F32)
-            grouped = work.tile([P, CHUNK * PACK], BF16, align_bytes=64, name="x_grouped")
-            grouped_words = grouped[:].bitcast(F32).rearrange("q (i b u) -> q i b u", i=ROW_TILES, u=2)
-            for half in range(2):
-                turned = tr_ps.tile([P, 2, 2, P], F32, name="turned")
-                for i in range(2):
-                    for u in range(2):
-                        start = (2 * half + i) * (H // 2) + u * P
-                        nc.tensor.transpose(turned[:, i, u, :], words[:, start : start + P], ident[:])
-                nc.scalar.copy(
-                    out=grouped_words[:, 2 * half : 2 * half + 2],
-                    in_=turned[:].rearrange("q i u b -> q i b u"),
-                )
-            x_grouped[c] = grouped
+            if bank == 0:
+                x_grouped[c] = xg.tile([P, CHUNK_ROWS[c] * PACK], BF16, align_bytes=64, name="x_grouped")
+            grouped_words = x_grouped[c][:].bitcast(F32).rearrange("q (i b u) -> q i b u", i=tiles, u=2)
+            first = 2 * bank
+            n = min(2, tiles - first)
+            turned = tr_ps.tile([P, 2, 2, P], F32, name="turned")
+            for i in range(n):
+                for u in range(2):
+                    start = (first + i) * (H // 2) + u * P
+                    nc.tensor.transpose(turned[:, i, u, :], words[:, start : start + P], ident[:])
+            copy(
+                out=grouped_words[:, first : first + n],
+                in_=turned[:, 0:n].rearrange("q i u b -> q i b u"),
+            )
+
+        def banks(c):
+            return (CHUNK_ROWS[c] + 2 * P - 1) // (2 * P)
+
+        def transpose_rows(c):
+            for bank in range(banks(c)):
+                transpose_bank(c, bank, nc.scalar.copy)
 
         def quantise_rows(c):
-            codes = ahead.tile([P, CHUNK], U32, align_bytes=64, name="x_codes")
-            scales = ahead.tile([P, CHUNK], U8, align_bytes=64, name="x_scales")
+            codes = ahead.tile([P, CHUNK_ROWS[c]], U32, align_bytes=64, name="x_codes")
+            scales = ahead.tile([P, CHUNK_ROWS[c]], U8, align_bytes=64, name="x_scales")
             nc.vector.quantize_mx(out=codes[:].bitcast(FP8X4), scales=scales[:], in_=x_grouped[c][:])
             x_codes[c], x_scales[c] = codes, scales
 
         def stage1(c):
-            plain = work.tile([P, PACK, CHUNK], BF16, name="h_plain")
+            plain = work.tile([P, PACK, CHUNK_ROWS[c]], BF16, name="h_plain")
             for t in range(PACK):
-                sums = s1_ps.tile([P, CHUNK], F32, name="sums1")
+                sums = s1_ps.tile([P, CHUNK_ROWS[c]], F32, name="sums1")
                 nc.tensor.matmul_mx(
                     out=sums[:],
                     lhsT=cw_codes[:, t * P : (t + 1) * P].bitcast(FP8X4),
@@ -230,7 +221,7 @@ def tile_quantumneuralnetwork_pb_t_kernel(tc, h3, q2_qw, q2_cw, q2_cb, w3, b3, o
             h_plain[c] = plain
 
         def regroup_hidden(c):
-            grouped = work.tile([P, CHUNK, PACK], BF16, align_bytes=64, name="h_grouped")
+            grouped = work.tile([P, CHUNK_ROWS[c], PACK], BF16, align_bytes=64, name="h_grouped")
             nc.vector.tensor_copy(
                 out=grouped[:].rearrange("p (c i) t -> p c t i", i=4),
                 in_=h_plain[c][:].rearrange("p t (c i) -> p c t i", i=4),
@@ -238,8 +229,8 @@ def tile_quantumneuralnetwork_pb_t_kernel(tc, h3, q2_qw, q2_cw, q2_cb, w3, b3, o
             h_grouped[c] = grouped
 
         def quantise_hidden(c):
-            codes = work.tile([P, CHUNK], U32, align_bytes=64, name="h_codes")
-            scales = work.tile([P, CHUNK], U8, align_bytes=64, name="h_scales")
+            codes = work.tile([P, CHUNK_ROWS[c]], U32, align_bytes=64, name="h_codes")
+            scales = work.tile([P, CHUNK_ROWS[c]], U8, align_bytes=64, name="h_scales")
             nc.vector.quantize_mx(
                 out=codes[:].bitcast(FP8X4),
                 scales=scales[:],
@@ -248,11 +239,13 @@ def tile_quantumneuralnetwork_pb_t_kernel(tc, h3, q2_qw, q2_cw, q2_cb, w3, b3, o
             h_codes[c], h_scales[c] = codes, scales
 
         def stage2(c):
+            tiles = CHUNK_ROWS[c] // P
             banks = []
-            for half in range(2):
+            for first in range(0, tiles, 2):
+                n = min(2, tiles - first)
                 sums = s2_ps.tile([P, 2, D_OUT], F32, name="sums2")
-                for i in range(2):
-                    cols = slice((2 * half + i) * P, (2 * half + i + 1) * P)
+                for i in range(n):
+                    cols = slice((first + i) * P, (first + i + 1) * P)
                     nc.tensor.matmul_mx(
                         out=sums[:, i, :],
                         lhsT=h_codes[c][:, cols].bitcast(FP8X4),
@@ -266,12 +259,14 @@ def tile_quantumneuralnetwork_pb_t_kernel(tc, h3, q2_qw, q2_cw, q2_cb, w3, b3, o
             sums2[c] = banks
 
         def add_bias(c):
-            y = work.tile([P, ROW_TILES, D_OUT], F32, name="y")
-            for half in range(2):
+            tiles = CHUNK_ROWS[c] // P
+            y = work.tile([P, tiles, D_OUT], F32, name="y")
+            for first in range(0, tiles, 2):
+                n = min(2, tiles - first)
                 nc.vector.tensor_tensor(
-                    out=y[:, 2 * half : 2 * half + 2, :],
-                    in0=sums2[c][half][:],
-                    in1=b3_f32[:].unsqueeze(1).to_broadcast([P, 2, D_OUT]),
+                    out=y[:, first : first + n, :],
+                    in0=sums2[c][first // 2][:, 0:n, :],
+                    in1=b3_f32[:].unsqueeze(1).to_broadcast([P, n, D_OUT]),
                     op=ALU.add,
                 )
             outputs[c] = y
@@ -282,28 +277,64 @@ def tile_quantumneuralnetwork_pb_t_kernel(tc, h3, q2_qw, q2_cw, q2_cb, w3, b3, o
                 out=y[:], in0=y[:], scalar1=F32_MAX, scalar2=0.0, op0=ALU.min, op1=ALU.max
             )
             nc.sync.dma_start(
-                out=out[c * CHUNK : (c + 1) * CHUNK, :].rearrange("(p i) n -> p i n", i=ROW_TILES),
+                out=out[CHUNK_STARTS[c] : CHUNK_STARTS[c] + CHUNK_ROWS[c], :].rearrange(
+                    "(p i) n -> p i n", i=CHUNK_ROWS[c] // P
+                ),
                 in_=y[:],
             )
 
-        for c in range(LEAD):
+        def regroup_cw(copy, t):
+            copy(out=cw_grouped[:, t], in_=cw_by_pass[:, t])
+
+        trig = sines_and_cosines(nc, small, qw_raw)
+        regroup_cw(nc.scalar.copy, 0)
+        regroup_cw(nc.vector.tensor_copy, 1)
+        transpose_rows(0)
+        bias = hidden_bias(
+            nc,
+            small,
+            trig,
+            cb_raw,
+            [
+                lambda: regroup_cw(nc.vector.tensor_copy, 2),
+                lambda: regroup_cw(nc.vector.tensor_copy, 3),
+                lambda: quantise_cw(0, 2),
+                lambda: quantise_cw(2, 4),
+                lambda: quantise_rows(0),
+            ],
+        )
+        for c in range(1, TR_LEAD):
             transpose_rows(c)
-        for c in range(LEAD - 1):
+        for c in range(1, Q_LEAD):
             quantise_rows(c)
+        def prepare_stage2():
+            nc.vector.tensor_copy(out=w3_grouped[:], in_=w3_raw[:].rearrange("p t n -> p n t"))
+            nc.gpsimd.tensor_copy(out=b3_f32[:], in_=b3_bf16[:])
+            nc.vector.quantize_mx(
+                out=w3_codes[:].bitcast(FP8X4),
+                scales=w3_scales[:],
+                in_=w3_grouped[:].rearrange("p n t -> p (n t)"),
+            )
+
         prepare_stage2()
         for r in range(-1, N_CHUNKS + 1):
+            new = r + 1 + TR_LEAD
             if r + 1 < N_CHUNKS:
                 stage1(r + 1)
-            if r + 1 + LEAD < N_CHUNKS:
-                transpose_rows(r + 1 + LEAD)
+            if new < N_CHUNKS:
+                transpose_bank(new, 0, nc.scalar.copy)
+                if banks(new) > 1 and not (r < 1):
+                    transpose_bank(new, 1, nc.scalar.copy)
             if 0 <= r - 1 < N_CHUNKS:
                 stage2(r - 1)
             if 0 <= r < N_CHUNKS:
                 regroup_hidden(r)
-            if r + LEAD < N_CHUNKS:
-                quantise_rows(r + LEAD)
+            if r + 1 + Q_LEAD < N_CHUNKS:
+                quantise_rows(r + 1 + Q_LEAD)
             if 0 <= r - 1 < N_CHUNKS:
                 add_bias(r - 1)
                 relu_and_store(r - 1)
             if 0 <= r < N_CHUNKS:
                 quantise_hidden(r)
+            if new < N_CHUNKS and banks(new) > 1 and r < 1:
+                transpose_bank(new, 1, nc.vector.tensor_copy)

@@ -132,12 +132,15 @@ def tile_quantumneuralnetwork_pb_t_kernel(tc, h3, q2_qw, q2_cw, q2_cb, w3, b3, o
         nc.gpsimd.memset(warm[:], 0.0)
         nc.scalar.activation(out=warm[:], in_=warm[:], func=ACT.Sin)
         w3_raw = weights.tile([P, PACK, D_OUT], BF16)
-        b3_bf16 = weights.tile([P, D_OUT], BF16)
+        b3_row = weights.tile([P, D_OUT], BF16)
+        nc.gpsimd.memset(b3_row[:], 0.0)
+        ones = weights.tile([P, P], BF16)
+        nc.gpsimd.memset(ones[:], 1.0)
         h3_rows = {}
         for c in range(N_CHUNKS):
-            if c == 2:
+            if c == 4:
                 nc.sync.dma_start(out=w3_raw[:], in_=w3.rearrange("(p t) n -> p t n", t=PACK))
-                nc.sync.dma_start(out=b3_bf16[:], in_=b3.partition_broadcast(P))
+                nc.sync.dma_start(out=b3_row[0:1, :], in_=b3.unsqueeze(0))
             tiles = CHUNK_ROWS[c] // P
             h3_sb = rows.tile([P, tiles * H], BF16, name="h3_sb")
             nc.sync.dma_start(
@@ -309,14 +312,15 @@ def tile_quantumneuralnetwork_pb_t_kernel(tc, h3, q2_qw, q2_cw, q2_cb, w3, b3, o
             quantise_rows(c)
         def prepare_stage2():
             nc.vector.tensor_copy(out=w3_grouped[:], in_=w3_raw[:].rearrange("p t n -> p n t"))
-            nc.gpsimd.tensor_copy(out=b3_f32[:], in_=b3_bf16[:])
+            b3_sums = s2_ps.tile([P, 2, D_OUT], F32, name="sums2")
+            nc.tensor.matmul(b3_sums[:, 0, :], lhsT=ones[:], rhs=b3_row[:], start=True, stop=True)
+            nc.vector.tensor_copy(out=b3_f32[:], in_=b3_sums[:, 0, :])
             nc.vector.quantize_mx(
                 out=w3_codes[:].bitcast(FP8X4),
                 scales=w3_scales[:],
                 in_=w3_grouped[:].rearrange("p n t -> p (n t)"),
             )
 
-        prepare_stage2()
         for r in range(-1, N_CHUNKS + 1):
             new = r + 1 + TR_LEAD
             if r + 1 < N_CHUNKS:
@@ -336,5 +340,7 @@ def tile_quantumneuralnetwork_pb_t_kernel(tc, h3, q2_qw, q2_cw, q2_cb, w3, b3, o
                 relu_and_store(r - 1)
             if 0 <= r < N_CHUNKS:
                 quantise_hidden(r)
+            if r == 0:
+                prepare_stage2()
             if new < N_CHUNKS and banks(new) > 1 and r < 1:
                 transpose_bank(new, 1, nc.vector.tensor_copy)

@@ -226,8 +226,8 @@ def tile_quantumneuralnetwork_pb_t_kernel(tc, h3, q2_qw, q2_cw, q2_cb, w3, b3, o
         def regroup_hidden(c):
             grouped = work.tile([P, CHUNK_ROWS[c], PACK], BF16, align_bytes=64, name="h_grouped")
             nc.vector.tensor_copy(
-                out=grouped[:].rearrange("p (c i) t -> p c t i", i=4),
-                in_=h_plain[c][:].rearrange("p t (c i) -> p c t i", i=4),
+                out=grouped[:].rearrange("p (c i) t -> p c t i", i=8),
+                in_=h_plain[c][:].rearrange("p t (c i) -> p c t i", i=8),
             )
             h_grouped[c] = grouped
 

@@ -15,9 +15,10 @@ ACT = mybir.ActivationFunctionType
 P = 128
 PACK = 4
 B, H, D_OUT, DEPTH = 8192, 512, 256, 3
-CHUNK_ROWS = [256, 256] + [512] * 14 + [256, 128, 128]
+CHUNK_ROWS = [256] + [512] * 15 + [256]
 N_CHUNKS = len(CHUNK_ROWS)
 CHUNK_STARTS = [sum(CHUNK_ROWS[:c]) for c in range(N_CHUNKS)]
+RELU_SCALAR = 128
 TR_LEAD = 2
 Q_LEAD = 1
 F32_MAX = 3.4028234663852886e38
@@ -138,7 +139,7 @@ def tile_quantumneuralnetwork_pb_t_kernel(tc, h3, q2_qw, q2_cw, q2_cb, w3, b3, o
         nc.gpsimd.memset(ones[:], 1.0)
         h3_rows = {}
         for c in range(N_CHUNKS):
-            if c == 4:
+            if c == 2:
                 nc.sync.dma_start(out=w3_raw[:], in_=w3.rearrange("(p t) n -> p t n", t=PACK))
                 nc.sync.dma_start(out=b3_row[0:1, :], in_=b3.unsqueeze(0))
             tiles = CHUNK_ROWS[c] // P
@@ -222,14 +223,25 @@ def tile_quantumneuralnetwork_pb_t_kernel(tc, h3, q2_qw, q2_cw, q2_cb, w3, b3, o
                     out=plain[:, t, :], in_=sums[:], func=ACT.Tanh, bias=bias[:, t : t + 1], scale=1.0
                 )
             h_plain[c] = plain
+            regroup_scalar(c)
+
+        def regroup_part(c, copy, first, last):
+            copy(
+                out=h_grouped[c][:, first:last, :].rearrange("p (c i) t -> p c t i", i=8),
+                in_=h_plain[c][:, :, first:last].rearrange("p t (c i) -> p c t i", i=8),
+            )
+
+        def share(c):
+            return 0
+
+        def regroup_scalar(c):
+            h_grouped[c] = work.tile([P, CHUNK_ROWS[c], PACK], BF16, align_bytes=64, name="h_grouped")
+            if share(c):
+                regroup_part(c, nc.scalar.copy, CHUNK_ROWS[c] - share(c), CHUNK_ROWS[c])
 
         def regroup_hidden(c):
-            grouped = work.tile([P, CHUNK_ROWS[c], PACK], BF16, align_bytes=64, name="h_grouped")
-            nc.vector.tensor_copy(
-                out=grouped[:].rearrange("p (c i) t -> p c t i", i=8),
-                in_=h_plain[c][:].rearrange("p t (c i) -> p c t i", i=8),
-            )
-            h_grouped[c] = grouped
+            if share(c) < CHUNK_ROWS[c]:
+                regroup_part(c, nc.vector.tensor_copy, 0, CHUNK_ROWS[c] - share(c))
 
         def quantise_hidden(c):
             codes = work.tile([P, CHUNK_ROWS[c]], U32, align_bytes=64, name="h_codes")
@@ -274,16 +286,20 @@ def tile_quantumneuralnetwork_pb_t_kernel(tc, h3, q2_qw, q2_cw, q2_cb, w3, b3, o
                 )
             outputs[c] = y
 
-        def relu_and_store(c):
-            y = outputs[c]
-            nc.gpsimd.tensor_scalar(
-                out=y[:], in0=y[:], scalar1=F32_MAX, scalar2=0.0, op0=ALU.min, op1=ALU.max
-            )
+        def relu_gpsimd(c):
+            y = outputs[c][:].rearrange("p i n -> p (i n)")
+            rest = y[:, RELU_SCALAR:]
+            nc.gpsimd.tensor_scalar(out=rest, in0=rest, scalar1=F32_MAX, scalar2=0.0, op0=ALU.min, op1=ALU.max)
+
+        def relu_scalar_and_store(c):
+            y = outputs[c][:].rearrange("p i n -> p (i n)")
+            part = y[:, :RELU_SCALAR]
+            nc.scalar.activation(out=part, in_=part, func=ACT.Relu)
             nc.sync.dma_start(
                 out=out[CHUNK_STARTS[c] : CHUNK_STARTS[c] + CHUNK_ROWS[c], :].rearrange(
-                    "(p i) n -> p i n", i=CHUNK_ROWS[c] // P
+                    "(p i) n -> p (i n)", i=CHUNK_ROWS[c] // P
                 ),
-                in_=y[:],
+                in_=y,
             )
 
         def regroup_cw(copy, t):
@@ -321,13 +337,13 @@ def tile_quantumneuralnetwork_pb_t_kernel(tc, h3, q2_qw, q2_cw, q2_cb, w3, b3, o
                 in_=w3_grouped[:].rearrange("p n t -> p (n t)"),
             )
 
-        for r in range(-1, N_CHUNKS + 1):
+        for r in range(-1, N_CHUNKS + 2):
             new = r + 1 + TR_LEAD
             if r + 1 < N_CHUNKS:
                 stage1(r + 1)
             if new < N_CHUNKS:
                 transpose_bank(new, 0, nc.scalar.copy)
-                if banks(new) > 1 and not (r < 1):
+                if banks(new) > 1:
                     transpose_bank(new, 1, nc.scalar.copy)
             if 0 <= r - 1 < N_CHUNKS:
                 stage2(r - 1)
@@ -337,10 +353,10 @@ def tile_quantumneuralnetwork_pb_t_kernel(tc, h3, q2_qw, q2_cw, q2_cb, w3, b3, o
                 quantise_rows(r + 1 + Q_LEAD)
             if 0 <= r - 1 < N_CHUNKS:
                 add_bias(r - 1)
-                relu_and_store(r - 1)
+                relu_gpsimd(r - 1)
+            if 0 <= r - 2 < N_CHUNKS:
+                relu_scalar_and_store(r - 2)
             if 0 <= r < N_CHUNKS:
                 quantise_hidden(r)
-            if r == 0:
+            if r == -1:
                 prepare_stage2()
-            if new < N_CHUNKS and banks(new) > 1 and r < 1:
-                transpose_bank(new, 1, nc.vector.tensor_copy)

@@ -232,7 +232,7 @@ def tile_quantumneuralnetwork_pb_t_kernel(tc, h3, q2_qw, q2_cw, q2_cb, w3, b3, o
             )
 
         def share(c):
-            return 0
+            return CHUNK_ROWS[c] // 2 if c >= N_CHUNKS - 2 else 0
 
         def regroup_scalar(c):
             h_grouped[c] = work.tile([P, CHUNK_ROWS[c], PACK], BF16, align_bytes=64, name="h_grouped")
@@ -343,7 +343,7 @@ def tile_quantumneuralnetwork_pb_t_kernel(tc, h3, q2_qw, q2_cw, q2_cb, w3, b3, o
                 stage1(r + 1)
             if new < N_CHUNKS:
                 transpose_bank(new, 0, nc.scalar.copy)
-                if banks(new) > 1:
+                if banks(new) > 1 and not (r < 1):
                     transpose_bank(new, 1, nc.scalar.copy)
             if 0 <= r - 1 < N_CHUNKS:
                 stage2(r - 1)
@@ -360,3 +360,5 @@ def tile_quantumneuralnetwork_pb_t_kernel(tc, h3, q2_qw, q2_cw, q2_cb, w3, b3, o
                 quantise_hidden(r)
             if r == -1:
                 prepare_stage2()
+            if new < N_CHUNKS and banks(new) > 1 and r < 1:
+                transpose_bank(new, 1, nc.vector.tensor_copy)

@@ -18,7 +18,6 @@ B, H, D_OUT, DEPTH = 8192, 512, 256, 3
 CHUNK_ROWS = [256] + [512] * 15 + [256]
 N_CHUNKS = len(CHUNK_ROWS)
 CHUNK_STARTS = [sum(CHUNK_ROWS[:c]) for c in range(N_CHUNKS)]
-RELU_SCALAR = 128
 TR_LEAD = 2
 Q_LEAD = 1
 F32_MAX = 3.4028234663852886e38
@@ -115,6 +114,7 @@ def tile_quantumneuralnetwork_pb_t_kernel(tc, h3, q2_qw, q2_cw, q2_cb, w3, b3, o
         ahead = ctx.enter_context(tc.tile_pool(name="ahead", bufs=Q_LEAD + 2))
         work = ctx.enter_context(tc.tile_pool(name="work", bufs=4))
         xg = ctx.enter_context(tc.tile_pool(name="xg", bufs=TR_LEAD + 2))
+        out_rows = ctx.enter_context(tc.tile_pool(name="out_rows", bufs=N_CHUNKS))
         tr_ps = ctx.enter_context(tc.psum_pool(name="tr_ps", bufs=2))
         s1_ps = ctx.enter_context(tc.psum_pool(name="s1_ps", bufs=4))
         s2_ps = ctx.enter_context(tc.psum_pool(name="s2_ps", bufs=2))
@@ -275,7 +275,7 @@ def tile_quantumneuralnetwork_pb_t_kernel(tc, h3, q2_qw, q2_cw, q2_cb, w3, b3, o
 
         def add_bias(c):
             tiles = CHUNK_ROWS[c] // P
-            y = work.tile([P, tiles, D_OUT], F32, name="y")
+            y = out_rows.tile([P, tiles, D_OUT], F32, name="y")
             for first in range(0, tiles, 2):
                 n = min(2, tiles - first)
                 nc.vector.tensor_tensor(
@@ -286,20 +286,19 @@ def tile_quantumneuralnetwork_pb_t_kernel(tc, h3, q2_qw, q2_cw, q2_cb, w3, b3, o
                 )
             outputs[c] = y
 
-        def relu_gpsimd(c):
-            y = outputs[c][:].rearrange("p i n -> p (i n)")
-            rest = y[:, RELU_SCALAR:]
-            nc.gpsimd.tensor_scalar(out=rest, in0=rest, scalar1=F32_MAX, scalar2=0.0, op0=ALU.min, op1=ALU.max)
-
-        def relu_scalar_and_store(c):
-            y = outputs[c][:].rearrange("p i n -> p (i n)")
-            part = y[:, :RELU_SCALAR]
-            nc.scalar.activation(out=part, in_=part, func=ACT.Relu)
+        def relu_and_store(c):
+            y = outputs[c]
+            if c < N_CHUNKS - 3:
+                nc.gpsimd.tensor_scalar(
+                    out=y[:], in0=y[:], scalar1=F32_MAX, scalar2=0.0, op0=ALU.min, op1=ALU.max
+                )
+            else:
+                nc.scalar.activation(out=y[:], in_=y[:], func=ACT.Relu)
             nc.sync.dma_start(
                 out=out[CHUNK_STARTS[c] : CHUNK_STARTS[c] + CHUNK_ROWS[c], :].rearrange(
-                    "(p i) n -> p (i n)", i=CHUNK_ROWS[c] // P
+                    "(p i) n -> p i n", i=CHUNK_ROWS[c] // P
                 ),
-                in_=y,
+                in_=y[:],
             )
 
         def regroup_cw(copy, t):
@@ -337,7 +336,7 @@ def tile_quantumneuralnetwork_pb_t_kernel(tc, h3, q2_qw, q2_cw, q2_cb, w3, b3, o
                 in_=w3_grouped[:].rearrange("p n t -> p (n t)"),
             )
 
-        for r in range(-1, N_CHUNKS + 2):
+        for r in range(-1, N_CHUNKS + 1):
             new = r + 1 + TR_LEAD
             if r + 1 < N_CHUNKS:
                 stage1(r + 1)
@@ -353,9 +352,7 @@ def tile_quantumneuralnetwork_pb_t_kernel(tc, h3, q2_qw, q2_cw, q2_cb, w3, b3, o
                 quantise_rows(r + 1 + Q_LEAD)
             if 0 <= r - 1 < N_CHUNKS:
                 add_bias(r - 1)
-                relu_gpsimd(r - 1)
-            if 0 <= r - 2 < N_CHUNKS:
-                relu_scalar_and_store(r - 2)
+                relu_and_store(r - 1)
             if 0 <= r < N_CHUNKS:
                 quantise_hidden(r)
             if r == -1:

@@ -206,24 +206,25 @@ def tile_quantumneuralnetwork_pb_t_kernel(tc, h3, q2_qw, q2_cw, q2_cb, w3, b3, o
             nc.vector.quantize_mx(out=codes[:].bitcast(FP8X4), scales=scales[:], in_=x_grouped[c][:])
             x_codes[c], x_scales[c] = codes, scales
 
-        def stage1(c):
-            plain = work.tile([P, PACK, CHUNK_ROWS[c]], BF16, name="h_plain")
-            for t in range(PACK):
-                sums = s1_ps.tile([P, CHUNK_ROWS[c]], F32, name="sums1")
-                nc.tensor.matmul_mx(
-                    out=sums[:],
-                    lhsT=cw_codes[:, t * P : (t + 1) * P].bitcast(FP8X4),
-                    lhsT_scale=cw_scales[:, t * P : (t + 1) * P],
-                    rhs=x_codes[c][:].bitcast(FP8X4),
-                    rhs_scale=x_scales[c][:],
-                    start=True,
-                    stop=True,
-                )
-                nc.scalar.activation(
-                    out=plain[:, t, :], in_=sums[:], func=ACT.Tanh, bias=bias[:, t : t + 1], scale=1.0
-                )
-            h_plain[c] = plain
-            regroup_scalar(c)
+        def stage1_pass(c, t):
+            if t == 0:
+                h_plain[c] = work.tile([P, PACK, CHUNK_ROWS[c]], BF16, name="h_plain")
+            plain = h_plain[c]
+            sums = s1_ps.tile([P, CHUNK_ROWS[c]], F32, name="sums1")
+            nc.tensor.matmul_mx(
+                out=sums[:],
+                lhsT=cw_codes[:, t * P : (t + 1) * P].bitcast(FP8X4),
+                lhsT_scale=cw_scales[:, t * P : (t + 1) * P],
+                rhs=x_codes[c][:].bitcast(FP8X4),
+                rhs_scale=x_scales[c][:],
+                start=True,
+                stop=True,
+            )
+            nc.scalar.activation(
+                out=plain[:, t, :], in_=sums[:], func=ACT.Tanh, bias=bias[:, t : t + 1], scale=1.0
+            )
+            if t == PACK - 1:
+                regroup_scalar(c)
 
         def regroup_part(c, copy, first, last):
             copy(
@@ -253,25 +254,23 @@ def tile_quantumneuralnetwork_pb_t_kernel(tc, h3, q2_qw, q2_cw, q2_cb, w3, b3, o
             )
             h_codes[c], h_scales[c] = codes, scales
 
-        def stage2(c):
+        def stage2_bank(c, bank):
             tiles = CHUNK_ROWS[c] // P
-            banks = []
-            for first in range(0, tiles, 2):
-                n = min(2, tiles - first)
-                sums = s2_ps.tile([P, 2, D_OUT], F32, name="sums2")
-                for i in range(n):
-                    cols = slice((first + i) * P, (first + i + 1) * P)
-                    nc.tensor.matmul_mx(
-                        out=sums[:, i, :],
-                        lhsT=h_codes[c][:, cols].bitcast(FP8X4),
-                        lhsT_scale=h_scales[c][:, cols],
-                        rhs=w3_codes[:].bitcast(FP8X4),
-                        rhs_scale=w3_scales[:],
-                        start=True,
-                        stop=True,
-                    )
-                banks.append(sums)
-            sums2[c] = banks
+            first = 2 * bank
+            n = min(2, tiles - first)
+            sums = s2_ps.tile([P, 2, D_OUT], F32, name="sums2")
+            for i in range(n):
+                cols = slice((first + i) * P, (first + i + 1) * P)
+                nc.tensor.matmul_mx(
+                    out=sums[:, i, :],
+                    lhsT=h_codes[c][:, cols].bitcast(FP8X4),
+                    lhsT_scale=h_scales[c][:, cols],
+                    rhs=w3_codes[:].bitcast(FP8X4),
+                    rhs_scale=w3_scales[:],
+                    start=True,
+                    stop=True,
+                )
+            sums2[c, bank] = sums
 
         def add_bias(c):
             tiles = CHUNK_ROWS[c] // P
@@ -280,7 +279,7 @@ def tile_quantumneuralnetwork_pb_t_kernel(tc, h3, q2_qw, q2_cw, q2_cb, w3, b3, o
                 n = min(2, tiles - first)
                 nc.vector.tensor_tensor(
                     out=y[:, first : first + n, :],
-                    in0=sums2[c][first // 2][:, 0:n, :],
+                    in0=sums2[c, first // 2][:, 0:n, :],
                     in1=b3_f32[:].unsqueeze(1).to_broadcast([P, n, D_OUT]),
                     op=ALU.add,
                 )
@@ -339,13 +338,21 @@ def tile_quantumneuralnetwork_pb_t_kernel(tc, h3, q2_qw, q2_cw, q2_cb, w3, b3, o
         for r in range(-1, N_CHUNKS + 1):
             new = r + 1 + TR_LEAD
             if r + 1 < N_CHUNKS:
-                stage1(r + 1)
+                stage1_pass(r + 1, 0)
+            if r + 1 < N_CHUNKS:
+                stage1_pass(r + 1, 1)
+            if 0 <= r - 1 < N_CHUNKS and banks(r - 1) > 0:
+                stage2_bank(r - 1, 0)
+            if 0 <= r - 1 < N_CHUNKS and banks(r - 1) > 1:
+                stage2_bank(r - 1, 1)
+            if r + 1 < N_CHUNKS:
+                stage1_pass(r + 1, 2)
+            if r + 1 < N_CHUNKS:
+                stage1_pass(r + 1, 3)
             if new < N_CHUNKS:
                 transpose_bank(new, 0, nc.scalar.copy)
-                if banks(new) > 1 and not (r < 1):
-                    transpose_bank(new, 1, nc.scalar.copy)
-            if 0 <= r - 1 < N_CHUNKS:
-                stage2(r - 1)
+            if new < N_CHUNKS and banks(new) > 1 and not (r < 1):
+                transpose_bank(new, 1, nc.scalar.copy)
             if 0 <= r < N_CHUNKS:
                 regroup_hidden(r)
             if r + 1 + Q_LEAD < N_CHUNKS:

@@ -32,17 +32,17 @@ HALF_BELOW = 0.4999999
 def sines_and_cosines(nc, small, qw_raw):
     angles = ((qw_raw[:, :, :, 0], 2.0 * INV_TWO_PI), (qw_raw[:, :, :, 3], INV_TWO_PI))
     shifted = small.tile([P, 2, DEPTH, PACK], F32)
+    in_turns = small.tile([P, 2, DEPTH, PACK], F32)
     for a, (raw, scale) in enumerate(angles):
         nc.vector.tensor_scalar(
             out=shifted[:, a], in0=raw, scalar1=scale, scalar2=ROUND_MAGIC, op0=ALU.mult, op1=ALU.add
         )
-    turns = small.tile([P, 2, DEPTH, PACK], F32)
-    nc.vector.tensor_scalar_sub(out=turns[:], in0=shifted[:], scalar1=ROUND_MAGIC)
-    part = small.tile([P, 2, DEPTH, PACK], F32)
     for a, (raw, scale) in enumerate(angles):
-        nc.vector.scalar_tensor_tensor(
-            out=part[:, a], in0=raw, scalar=scale, in1=turns[:, a], op0=ALU.mult, op1=ALU.subtract
-        )
+        nc.vector.tensor_scalar_mul(out=in_turns[:, a], in0=raw, scalar1=scale)
+    part = small.tile([P, 2, DEPTH, PACK], F32)
+    nc.vector.scalar_tensor_tensor(
+        out=part[:], in0=shifted[:], scalar=ROUND_MAGIC, in1=in_turns[:], op0=ALU.subtract, op1=ALU.subtract
+    )
     clipped = small.tile([P, 2, DEPTH, PACK], F32)
     nc.vector.tensor_scalar(
         out=clipped[:], in0=part[:], scalar1=HALF_BELOW, scalar2=-HALF_BELOW, op0=ALU.min, op1=ALU.max
@@ -52,7 +52,7 @@ def sines_and_cosines(nc, small, qw_raw):
         out=size[:], in0=part[:], scalar=-1.0, in1=part[:], op0=ALU.mult, op1=ALU.max
     )
     trig = small.tile([P, 2, 2, DEPTH, PACK], F32)
-    nc.scalar.activation(out=trig[:, 0], in_=clipped[:], func=ACT.Sin, scale=2.0 * math.pi)
+    nc.scalar.activation(out=trig[:, 0], in_=clipped[:], func=ACT.Sin, scale=-2.0 * math.pi)
     nc.scalar.activation(
         out=trig[:, 1], in_=size[:], func=ACT.Sin, scale=-2.0 * math.pi, bias=math.pi / 2
     )
@@ -316,8 +316,8 @@ def tile_quantumneuralnetwork_pb_t_kernel(tc, h3, q2_qw, q2_cw, q2_cb, w3, b3, o
                 lambda: regroup_cw(nc.vector.tensor_copy, 2),
                 lambda: regroup_cw(nc.vector.tensor_copy, 3),
                 lambda: quantise_cw(0, 2),
-                lambda: quantise_cw(2, 4),
                 lambda: quantise_rows(0),
+                lambda: quantise_cw(2, 4),
             ],
         )
         for c in range(1, TR_LEAD):

import math
from contextlib import ExitStack

import concourse.mybir as mybir
from concourse.masks import make_identity

F32 = mybir.dt.float32
BF16 = mybir.dt.bfloat16
U32 = mybir.dt.uint32
U8 = mybir.dt.uint8
FP8X4 = mybir.dt.float8_e4m3fn_x4
ALU = mybir.AluOpType
ACT = mybir.ActivationFunctionType

P = 128
PACK = 4
B, H, D_OUT, DEPTH = 8192, 512, 256, 3
CHUNK_ROWS = [256] + [512] * 15 + [256]
N_CHUNKS = len(CHUNK_ROWS)
CHUNK_STARTS = [sum(CHUNK_ROWS[:c]) for c in range(N_CHUNKS)]
TR_LEAD = 2
Q_LEAD = 1
F32_MAX = 3.4028234663852886e38

FLOPS = 2 * B * H * (H + D_OUT)

INV_TWO_PI = 1.0 / (2.0 * math.pi)
ROUND_MAGIC = 12582912.0
HALF_BELOW = 0.4999999


def sines_and_cosines(nc, small, qw_raw):
    angles = ((qw_raw[:, :, :, 0], 2.0 * INV_TWO_PI), (qw_raw[:, :, :, 3], INV_TWO_PI))
    shifted = small.tile([P, 2, DEPTH, PACK], F32)
    in_turns = small.tile([P, 2, DEPTH, PACK], F32)
    for a, (raw, scale) in enumerate(angles):
        nc.vector.tensor_scalar(
            out=shifted[:, a], in0=raw, scalar1=scale, scalar2=ROUND_MAGIC, op0=ALU.mult, op1=ALU.add
        )
    for a, (raw, scale) in enumerate(angles):
        nc.vector.tensor_scalar_mul(out=in_turns[:, a], in0=raw, scalar1=scale)
    part = small.tile([P, 2, DEPTH, PACK], F32)
    nc.vector.scalar_tensor_tensor(
        out=part[:], in0=shifted[:], scalar=ROUND_MAGIC, in1=in_turns[:], op0=ALU.subtract, op1=ALU.subtract
    )
    clipped = small.tile([P, 2, DEPTH, PACK], F32)
    nc.vector.tensor_scalar(
        out=clipped[:], in0=part[:], scalar1=HALF_BELOW, scalar2=-HALF_BELOW, op0=ALU.min, op1=ALU.max
    )
    size = small.tile([P, 2, DEPTH, PACK], F32)
    nc.vector.scalar_tensor_tensor(
        out=size[:], in0=part[:], scalar=-1.0, in1=part[:], op0=ALU.mult, op1=ALU.max
    )
    trig = small.tile([P, 2, 2, DEPTH, PACK], F32)
    nc.scalar.activation(out=trig[:, 0], in_=clipped[:], func=ACT.Sin, scale=-2.0 * math.pi)
    nc.scalar.activation(
        out=trig[:, 1], in_=size[:], func=ACT.Sin, scale=-2.0 * math.pi, bias=math.pi / 2
    )
    return trig


def hidden_bias(nc, small, trig, cb_raw, between):
    cb_half = small.tile([P, PACK], F32)
    nc.gpsimd.tensor_scalar(
        out=cb_half[:], in0=cb_raw[:], scalar1=1.0, scalar2=0.5, op0=ALU.mult, op1=ALU.add
    )
    xk = small.tile([P, 2, 2, PACK], F32)
    nc.vector.tensor_tensor(
        out=xk[:],
        in0=trig[:, 0, 0, 0:3:2, :].unsqueeze(1).to_broadcast([P, 2, 2, PACK]),
        in1=trig[:, :, 1, 0:2, :],
        op=ALU.mult,
    )
    turn = trig[:, :, 0, 1, :]
    by_z = small.tile([P, 2, PACK], F32)
    nc.vector.tensor_tensor(
        out=by_z[:], in0=turn, in1=trig[:, 1, 0, 0, :].unsqueeze(1).to_broadcast([P, 2, PACK]), op=ALU.mult
    )
    between[0]()
    by_x = small.tile([P, 2, PACK], F32)
    nc.vector.tensor_tensor(
        out=by_x[:], in0=turn, in1=xk[:, 1, 0, :].unsqueeze(1).to_broadcast([P, 2, PACK]), op=ALU.mult
    )
    between[1]()
    z1 = small.tile([P, PACK], F32)
    nc.vector.tensor_tensor(out=z1[:], in0=by_z[:, 1, :], in1=by_x[:, 0, :], op=ALU.subtract)
    minus_x1 = xk[:, 1, 0, :]
    nc.vector.scalar_tensor_tensor(
        out=minus_x1, in0=by_z[:, 0, :], scalar=-1.0, in1=by_x[:, 1, :], op0=ALU.mult, op1=ALU.subtract
    )
    between[2]()
    terms = small.tile([P, 3, PACK], F32)
    nc.vector.tensor_tensor(out=terms[:, 2, :], in0=z1[:], in1=trig[:, 1, 0, 2, :], op=ALU.mult)
    nc.vector.tensor_tensor(out=terms[:, 0:2, :], in0=xk[:, :, 0, :], in1=xk[:, :, 1, :], op=ALU.mult)
    between[3]()
    z2 = small.tile([P, PACK], F32)
    nc.vector.tensor_reduce(
        out=z2[:], in_=terms[:].rearrange("p j t -> p t j"), axis=mybir.AxisListType.X, op=ALU.add
    )
    between[4]()
    bias = small.tile([P, PACK], F32)
    nc.vector.scalar_tensor_tensor(
        out=bias[:], in0=z2[:], scalar=0.5, in1=cb_half[:], op0=ALU.mult, op1=ALU.add
    )
    return bias


def tile_quantumneuralnetwork_pb_t_kernel(tc, h3, q2_qw, q2_cw, q2_cb, w3, b3, out):
    nc = tc.nc
    with ExitStack() as ctx:
        small = ctx.enter_context(tc.tile_pool(name="small", bufs=1))
        weights = ctx.enter_context(tc.tile_pool(name="weights", bufs=1))
        rows = ctx.enter_context(tc.tile_pool(name="rows", bufs=N_CHUNKS))
        ahead = ctx.enter_context(tc.tile_pool(name="ahead", bufs=Q_LEAD + 2))
        work = ctx.enter_context(tc.tile_pool(name="work", bufs=4))
        xg = ctx.enter_context(tc.tile_pool(name="xg", bufs=TR_LEAD + 2))
        out_rows = ctx.enter_context(tc.tile_pool(name="out_rows", bufs=N_CHUNKS))
        tr_ps = ctx.enter_context(tc.psum_pool(name="tr_ps", bufs=2))
        s1_ps = ctx.enter_context(tc.psum_pool(name="s1_ps", bufs=4))
        s2_ps = ctx.enter_context(tc.psum_pool(name="s2_ps", bufs=2))
        ctx.enter_context(tc.manual_schedule())

        qw_raw = small.tile([P, DEPTH, PACK, 4], BF16)
        nc.sync.dma_start(out=qw_raw[:], in_=q2_qw.rearrange("d (p t) a b -> p d t (a b)", t=PACK))
        cb_raw = small.tile([P, PACK], BF16)
        cw_raw = weights.tile([P, PACK, H], BF16)
        nc.scalar.dma_start(
            out=cw_raw[:].rearrange("q (u e) n -> q u (e n)", u=2),
            in_=q2_cw.rearrange("(u q e) n -> q u (e n)", u=2, e=2),
        )
        nc.scalar.dma_start(out=cb_raw[:], in_=q2_cb.rearrange("(p t) -> p t", t=PACK))
        warm = small.tile([P, 1], F32)
        nc.gpsimd.memset(warm[:], 0.0)
        nc.scalar.activation(out=warm[:], in_=warm[:], func=ACT.Sin)
        w3_raw = weights.tile([P, PACK, D_OUT], BF16)
        b3_row = weights.tile([P, D_OUT], BF16)
        nc.gpsimd.memset(b3_row[:], 0.0)
        ones = weights.tile([P, P], BF16)
        nc.gpsimd.memset(ones[:], 1.0)
        h3_rows = {}
        for c in range(N_CHUNKS):
            if c == 2:
                nc.sync.dma_start(out=w3_raw[:], in_=w3.rearrange("(p t) n -> p t n", t=PACK))
                nc.sync.dma_start(out=b3_row[0:1, :], in_=b3.unsqueeze(0))
            tiles = CHUNK_ROWS[c] // P
            h3_sb = rows.tile([P, tiles * H], BF16, name="h3_sb")
            nc.sync.dma_start(
                out=h3_sb[:],
                in_=h3[CHUNK_STARTS[c] : CHUNK_STARTS[c] + CHUNK_ROWS[c], :].rearrange(
                    "(p i) k -> p (i k)", i=tiles
                ),
            )
            h3_rows[c] = h3_sb

        ident = weights.tile([P, P], F32)
        make_identity(nc, ident[:])

        cw_grouped = weights.tile([P, PACK, P, PACK], BF16, align_bytes=64)
        cw_by_pass = cw_raw[:].rearrange("q k (c t) -> q t c k", t=PACK)
        cw_codes = weights.tile([P, H], U32, align_bytes=64)
        cw_scales = weights.tile([P, H], U8, align_bytes=64)
        w3_grouped = weights.tile([P, D_OUT, PACK], BF16, align_bytes=64)
        w3_codes = weights.tile([P, D_OUT], U32, align_bytes=64)
        w3_scales = weights.tile([P, D_OUT], U8, align_bytes=64)
        b3_f32 = weights.tile([P, D_OUT], F32)

        def quantise_cw(first, last):
            nc.vector.quantize_mx(
                out=cw_codes[:, first * P : last * P].bitcast(FP8X4),
                scales=cw_scales[:, first * P : last * P],
                in_=cw_grouped[:, first:last].rearrange("q t c k -> q (t c k)"),
            )

        x_grouped, x_codes, x_scales = {}, {}, {}
        h_plain, h_grouped, h_codes, h_scales = {}, {}, {}, {}
        sums2, outputs = {}, {}

        def transpose_bank(c, bank, copy):
            tiles = CHUNK_ROWS[c] // P
            words = h3_rows[c][:].bitcast(F32)
            if bank == 0:
                x_grouped[c] = xg.tile([P, CHUNK_ROWS[c] * PACK], BF16, align_bytes=64, name="x_grouped")
            grouped_words = x_grouped[c][:].bitcast(F32).rearrange("q (i b u) -> q i b u", i=tiles, u=2)
            first = 2 * bank
            n = min(2, tiles - first)
            turned = tr_ps.tile([P, 2, 2, P], F32, name="turned")
            for i in range(n):
                for u in range(2):
                    start = (first + i) * (H // 2) + u * P
                    nc.tensor.transpose(turned[:, i, u, :], words[:, start : start + P], ident[:])
            copy(
                out=grouped_words[:, first : first + n],
                in_=turned[:, 0:n].rearrange("q i u b -> q i b u"),
            )

        def banks(c):
            return (CHUNK_ROWS[c] + 2 * P - 1) // (2 * P)

        def transpose_rows(c):
            for bank in range(banks(c)):
                transpose_bank(c, bank, nc.scalar.copy)

        def quantise_rows(c):
            codes = ahead.tile([P, CHUNK_ROWS[c]], U32, align_bytes=64, name="x_codes")
            scales = ahead.tile([P, CHUNK_ROWS[c]], U8, align_bytes=64, name="x_scales")
            nc.vector.quantize_mx(out=codes[:].bitcast(FP8X4), scales=scales[:], in_=x_grouped[c][:])
            x_codes[c], x_scales[c] = codes, scales

        def stage1_pass(c, t):
            if t == 0:
                h_plain[c] = work.tile([P, PACK, CHUNK_ROWS[c]], BF16, name="h_plain")
            plain = h_plain[c]
            sums = s1_ps.tile([P, CHUNK_ROWS[c]], F32, name="sums1")
            nc.tensor.matmul_mx(
                out=sums[:],
                lhsT=cw_codes[:, t * P : (t + 1) * P].bitcast(FP8X4),
                lhsT_scale=cw_scales[:, t * P : (t + 1) * P],
                rhs=x_codes[c][:].bitcast(FP8X4),
                rhs_scale=x_scales[c][:],
                start=True,
                stop=True,
            )
            nc.scalar.activation(
                out=plain[:, t, :], in_=sums[:], func=ACT.Tanh, bias=bias[:, t : t + 1], scale=1.0
            )
            if t == PACK - 1:
                regroup_scalar(c)

        def regroup_part(c, copy, first, last):
            copy(
                out=h_grouped[c][:, first:last, :].rearrange("p (c i) t -> p c t i", i=8),
                in_=h_plain[c][:, :, first:last].rearrange("p t (c i) -> p c t i", i=8),
            )

        def share(c):
            return CHUNK_ROWS[c] // 2 if c >= N_CHUNKS - 2 else 0

        def regroup_scalar(c):
            h_grouped[c] = work.tile([P, CHUNK_ROWS[c], PACK], BF16, align_bytes=64, name="h_grouped")
            if share(c):
                regroup_part(c, nc.scalar.copy, CHUNK_ROWS[c] - share(c), CHUNK_ROWS[c])

        def regroup_hidden(c):
            if share(c) < CHUNK_ROWS[c]:
                regroup_part(c, nc.vector.tensor_copy, 0, CHUNK_ROWS[c] - share(c))

        def quantise_hidden(c):
            codes = work.tile([P, CHUNK_ROWS[c]], U32, align_bytes=64, name="h_codes")
            scales = work.tile([P, CHUNK_ROWS[c]], U8, align_bytes=64, name="h_scales")
            nc.vector.quantize_mx(
                out=codes[:].bitcast(FP8X4),
                scales=scales[:],
                in_=h_grouped[c][:].rearrange("p b t -> p (b t)"),
            )
            h_codes[c], h_scales[c] = codes, scales

        def stage2_bank(c, bank):
            tiles = CHUNK_ROWS[c] // P
            first = 2 * bank
            n = min(2, tiles - first)
            sums = s2_ps.tile([P, 2, D_OUT], F32, name="sums2")
            for i in range(n):
                cols = slice((first + i) * P, (first + i + 1) * P)
                nc.tensor.matmul_mx(
                    out=sums[:, i, :],
                    lhsT=h_codes[c][:, cols].bitcast(FP8X4),
                    lhsT_scale=h_scales[c][:, cols],
                    rhs=w3_codes[:].bitcast(FP8X4),
                    rhs_scale=w3_scales[:],
                    start=True,
                    stop=True,
                )
            sums2[c, bank] = sums

        def add_bias(c):
            tiles = CHUNK_ROWS[c] // P
            y = out_rows.tile([P, tiles, D_OUT], F32, name="y")
            for first in range(0, tiles, 2):
                n = min(2, tiles - first)
                nc.vector.tensor_tensor(
                    out=y[:, first : first + n, :],
                    in0=sums2[c, first // 2][:, 0:n, :],
                    in1=b3_f32[:].unsqueeze(1).to_broadcast([P, n, D_OUT]),
                    op=ALU.add,
                )
            outputs[c] = y

        def relu_and_store(c):
            y = outputs[c]
            if c < N_CHUNKS - 3:
                nc.gpsimd.tensor_scalar(
                    out=y[:], in0=y[:], scalar1=F32_MAX, scalar2=0.0, op0=ALU.min, op1=ALU.max
                )
            else:
                nc.scalar.activation(out=y[:], in_=y[:], func=ACT.Relu)
            nc.sync.dma_start(
                out=out[CHUNK_STARTS[c] : CHUNK_STARTS[c] + CHUNK_ROWS[c], :].rearrange(
                    "(p i) n -> p i n", i=CHUNK_ROWS[c] // P
                ),
                in_=y[:],
            )

        def regroup_cw(copy, t):
            copy(out=cw_grouped[:, t], in_=cw_by_pass[:, t])

        trig = sines_and_cosines(nc, small, qw_raw)
        regroup_cw(nc.scalar.copy, 0)
        regroup_cw(nc.vector.tensor_copy, 1)
        transpose_rows(0)
        bias = hidden_bias(
            nc,
            small,
            trig,
            cb_raw,
            [
                lambda: regroup_cw(nc.vector.tensor_copy, 2),
                lambda: regroup_cw(nc.vector.tensor_copy, 3),
                lambda: quantise_cw(0, 2),
                lambda: quantise_rows(0),
                lambda: quantise_cw(2, 4),
            ],
        )
        for c in range(1, TR_LEAD):
            transpose_rows(c)
        for c in range(1, Q_LEAD):
            quantise_rows(c)
        def prepare_stage2():
            nc.vector.tensor_copy(out=w3_grouped[:], in_=w3_raw[:].rearrange("p t n -> p n t"))
            b3_sums = s2_ps.tile([P, 2, D_OUT], F32, name="sums2")
            nc.tensor.matmul(b3_sums[:, 0, :], lhsT=ones[:], rhs=b3_row[:], start=True, stop=True)
            nc.vector.tensor_copy(out=b3_f32[:], in_=b3_sums[:, 0, :])
            nc.vector.quantize_mx(
                out=w3_codes[:].bitcast(FP8X4),
                scales=w3_scales[:],
                in_=w3_grouped[:].rearrange("p n t -> p (n t)"),
            )

        for r in range(-1, N_CHUNKS + 1):
            new = r + 1 + TR_LEAD
            if r + 1 < N_CHUNKS:
                stage1_pass(r + 1, 0)
            if r + 1 < N_CHUNKS:
                stage1_pass(r + 1, 1)
            if 0 <= r - 1 < N_CHUNKS and banks(r - 1) > 0:
                stage2_bank(r - 1, 0)
            if 0 <= r - 1 < N_CHUNKS and banks(r - 1) > 1:
                stage2_bank(r - 1, 1)
            if r + 1 < N_CHUNKS:
                stage1_pass(r + 1, 2)
            if r + 1 < N_CHUNKS:
                stage1_pass(r + 1, 3)
            if new < N_CHUNKS:
                transpose_bank(new, 0, nc.scalar.copy)
            if new < N_CHUNKS and banks(new) > 1 and not (r < 1):
                transpose_bank(new, 1, nc.scalar.copy)
            if 0 <= r < N_CHUNKS:
                regroup_hidden(r)
            if r + 1 + Q_LEAD < N_CHUNKS:
                quantise_rows(r + 1 + Q_LEAD)
            if 0 <= r - 1 < N_CHUNKS:
                add_bias(r - 1)
                relu_and_store(r - 1)
            if 0 <= r < N_CHUNKS:
                quantise_hidden(r)
            if r == -1:
                prepare_stage2()
            if new < N_CHUNKS and banks(new) > 1 and r < 1:
                transpose_bank(new, 1, nc.vector.tensor_copy)
